import numpy as np
import ml_dtypes


def mxq(x, axis, fmt="e4m3"):
    dtype, down = {"e4m3": (ml_dtypes.float8_e4m3fn, 7), "e5m2": (ml_dtypes.float8_e5m2, 14)}[fmt]
    v = np.moveaxis(np.asarray(x, np.float32).astype(ml_dtypes.bfloat16).astype(np.float64), axis, -1)
    blocks = v.reshape(v.shape[:-1] + (-1, 32))
    amax = np.abs(blocks).max(-1, keepdims=True)
    byte = np.maximum(np.where(amax > 0, np.frexp(amax)[1] - 1 + 127, 0) - down, 1)
    scale = np.exp2(byte - 127.0)
    codes = (blocks / scale).astype(np.float32).astype(dtype).astype(np.float64)
    return np.moveaxis((codes * scale).reshape(v.shape), -1, axis)


WIDE = False


def mx_kscale(k):
    if not WIDE:
        return np.ones(k)
    levels = np.array([10, -10, 5, -5, 0])
    a = np.random.permutation(np.resize(levels, k // 512 * 4)).reshape(k // 512, 4)
    idx = np.arange(k)
    return np.exp2(a[idx // 512, idx % 128 // 32])


BF16 = ml_dtypes.bfloat16


def bf(x):
    return np.asarray(x, np.float32).astype(BF16)


def f64(x):
    return np.asarray(x).astype(np.float64)


B, C, F, T, H, W = 4, 512, 512, 8, 16, 16
N = T * H * W
BN_EPS = 1e-5


def setup_inputs():
    t = mx_kscale(F)
    return {"inputs": bf(np.random.standard_normal((B, C, T, H, W))),
            "Wv": bf(np.random.standard_normal((F, C)) / np.sqrt(C) * t[:, None]),
            "bv": bf(np.random.standard_normal(F) * 0.3 * t),
            "row": bf(1.0 + 0.1 * np.random.standard_normal((B, N))),
            "Wo": bf(np.random.standard_normal((C, F)) * 1.5 / np.sqrt(F) / t[None, :]),
            "bo": bf(np.random.standard_normal(C) * 0.3),
            "gamma": bf(1.0 + 0.1 * np.random.standard_normal(C)),
            "beta": bf(np.random.standard_normal(C) * 0.1)}


def reference(inputs, Wv, bv, row, Wo, bo, gamma, beta):
    x = f64(inputs).reshape(B, C, N)
    V = (mxq(f64(Wv), 1, "e4m3") @ mxq(x, 1, "e4m3")) + f64(bv)[None, :, None]
    V1 = np.maximum(V * f64(row)[:, None, :], 0.0)
    out = (mxq(f64(Wo), 1, "e4m3") @ mxq(V1, 1, "e4m3")) + f64(bo)[None, :, None]
    res = x + np.maximum(out, 0.0)
    mean = res.mean(axis=(0, -1), keepdims=True)
    var = res.var(axis=(0, -1), keepdims=True)
    xhat = (res - mean) / np.sqrt(var + BN_EPS)
    y = f64(gamma)[None, :, None] * xhat + f64(beta)[None, :, None]
    return y.reshape(B, C, T, H, W)

@@ -1,0 +1,303 @@
+from contextlib import ExitStack
+
+import concourse.mybir as mybir
+from concourse.masks import make_identity
+
+FLOPS = 2 * 2 * 512 * 512 * 8192
+
+BF16 = mybir.dt.bfloat16
+F32 = mybir.dt.float32
+U32 = mybir.dt.uint32
+U8 = mybir.dt.uint8
+FP8X4 = mybir.dt.float8_e4m3fn_x4
+ALU = mybir.AluOpType
+ACT = mybir.ActivationFunctionType
+AX = mybir.AxisListType
+
+P = 128
+PACK = 4
+B = 4
+N = 2048
+CH = 512
+QB = N // CH
+NCHUNK = B * QB
+NT = B * N
+EPS = 1e-5
+
+HB = 1024
+NHB = NT // HB
+X_ON_VECTOR = (1, 5, 9, 13)
+WO_AT = 2
+LEAD = 4
+
+
+def tile_nonlocallayer_pa_t_kernel(tc, inputs, Wv, bv, row, Wo, bo, gamma, beta, out):
+    nc = tc.nc
+    xv = inputs.rearrange("b (p j) t h w -> b p j (t h w)", j=PACK)
+    ov = out.rearrange("b (p j) t h w -> b p j (t h w)", j=PACK)
+
+    with ExitStack() as ctx:
+        keep = ctx.enter_context(tc.tile_pool(name="keep", bufs=1))
+        work = ctx.enter_context(tc.tile_pool(name="work", bufs=2))
+        resp = ctx.enter_context(tc.tile_pool(name="resp", bufs=17))
+        stat = ctx.enter_context(tc.tile_pool(name="stat", bufs=2))
+        psum = ctx.enter_context(tc.psum_pool(name="psum", bufs=8))
+        ctx.enter_context(tc.manual_schedule())
+
+        x_sb = keep.tile([P, B, PACK, N], BF16, name="x_sb")
+        rowb = keep.tile([P, B, N], BF16, name="rowb")
+        vq = keep.tile([P, NT], U32, name="vq", align_bytes=64)
+        vs = keep.tile([P, NT], U8, name="vs", align_bytes=64)
+        wq = [keep.tile([P, 512], U32, name="wq%d" % s, align_bytes=64) for s in range(2)]
+        ws = [keep.tile([P, 512], U8, name="ws%d" % s, align_bytes=64) for s in range(2)]
+        ident = keep.tile([P, P], F32, name="ident")
+        bv_b = keep.tile([P, PACK], BF16, name="bv_b")
+        bo_b = keep.tile([P, PACK], BF16, name="bo_b")
+        ga_b = keep.tile([P, PACK], BF16, name="ga_b")
+        be_b = keep.tile([P, PACK], BF16, name="be_b")
+        bv_f = keep.tile([P, PACK], F32, name="bv_f")
+        negbo = keep.tile([P, PACK], F32, name="negbo")
+        minbo = keep.tile([P, PACK], F32, name="minbo")
+        ga_f = keep.tile([P, PACK], F32, name="ga_f")
+        be_f = keep.tile([P, PACK], F32, name="be_f")
+        sums = keep.tile([P, PACK, NCHUNK], F32, name="sums")
+        sqs = keep.tile([P, PACK, NHB + 1], F32, name="sqs")
+        one = keep.tile([P, 1], F32, name="one")
+        one_s = keep.tile([P, 1], F32, name="one_s")
+
+        nc.vector.memset(one[:], 1.0)
+        nc.scalar.activation(out=one_s[:], in_=one[:], func=ACT.Sqrt)
+        make_identity(nc, ident[:])
+
+        raw = [resp.tile([P, HB], F32, name="raw%d" % s, tag="res") for s in range(2)]
+
+        def load_x(b, c0, c1):
+            nc.sync.dma_start(out=x_sb[:, b, :, c0:c1], in_=xv[b][:, :, c0:c1])
+
+        def load_row(b, c0, c1):
+            nc.sync.dma_start(out=rowb[:, b, c0:c1], in_=row[b, c0:c1].partition_broadcast(P))
+
+        def load_vec(dst, src):
+            nc.sync.dma_start(out=dst[:], in_=src.rearrange("(p i) -> p i", i=PACK))
+
+        def load_w(s, w):
+            nc.sync.dma_start(out=raw[s][:].bitcast(BF16).rearrange("p (i c) -> p i c", i=PACK),
+                              in_=w.rearrange("(m i) c -> m i c", i=PACK))
+
+        load_w(0, Wv)
+        load_x(0, 0, CH)
+        load_vec(bv_b, bv)
+        load_row(0, 0, CH)
+        load_x(0, CH, 2 * CH)
+        load_x(0, 2 * CH, N)
+        load_row(0, CH, N)
+        load_w(1, Wo)
+        load_vec(bo_b, bo)
+        load_vec(ga_b, gamma)
+        load_vec(be_b, beta)
+        for b in range(1, B):
+            load_x(b, 0, N)
+            load_row(b, 0, N)
+
+        wps = {}
+        wg = {}
+
+        def w_transpose(s):
+            words = raw[s][:].rearrange("p (i q u) -> p i u q", i=PACK, u=2)
+            for h in range(2):
+                ps = psum.tile([P, 512], F32, name="pst", tag="ps")
+                wps[(s, h)] = ps[:].rearrange("p (i u m) -> p i u m", i=2, u=2)
+                for i2 in range(2):
+                    for u in range(2):
+                        nc.tensor.transpose(wps[(s, h)][:, i2, u, :], words[:, 2 * h + i2, u, :], ident[:])
+
+        def w_copy(s):
+            wg[s] = work.tile([P, PACK * 512], BF16, name="gw%d" % s, tag="gv", align_bytes=64)
+            g4 = wg[s][:].bitcast(F32).rearrange("p (h i m u) -> p h i m u", h=2, i=2, u=2)
+            for h in range(2):
+                nc.vector.tensor_copy(out=g4[:, h], in_=wps[(s, h)].rearrange("p i u m -> p i m u"))
+
+        def w_quant(s):
+            nc.vector.quantize_mx(out=wq[s][:].bitcast(FP8X4), scales=ws[s][:], in_=wg[s][:])
+
+        gx = {}
+        xq = {}
+        ps1 = {}
+        zt = {}
+        gv = {}
+
+        def where(k):
+            b, q = divmod(k, QB)
+            return b, slice(q * CH, (q + 1) * CH)
+
+        def grouped_view(dst):
+            return dst.rearrange("p (c i t) -> p c t i", i=4, t=PACK)
+
+        def rows_view(src):
+            return src.rearrange("p t (c i) -> p c t i", i=4)
+
+        def regroup_x(k):
+            b, cols = where(k)
+            gx[k] = work.tile([P, PACK * CH], BF16, name="gx", align_bytes=64)
+            if k in X_ON_VECTOR:
+                nc.vector.tensor_copy(out=grouped_view(gx[k][:]), in_=rows_view(x_sb[:, b, :, cols]))
+            else:
+                nc.scalar.copy(out=grouped_view(gx[k][:]), in_=rows_view(x_sb[:, b, :, cols]))
+
+        def quant_x(k):
+            codes = work.tile([P, CH], U32, name="xq", align_bytes=64)
+            scales = work.tile([P, CH], U8, name="xs", align_bytes=64)
+            xq[k] = (codes, scales)
+            nc.vector.quantize_mx(out=codes[:].bitcast(FP8X4), scales=scales[:], in_=gx[k][:])
+
+        def matmul_1(k):
+            codes, scales = xq[k]
+            ps1[k] = []
+            for t in range(PACK):
+                ps = psum.tile([P, CH], F32, name="ps1", tag="ps")
+                ps1[k].append(ps)
+                nc.tensor.matmul_mx(out=ps[:], lhsT=wq[0][:, t * P:(t + 1) * P].bitcast(FP8X4),
+                                    lhsT_scale=ws[0][:, t * P:(t + 1) * P],
+                                    rhs=codes[:].bitcast(FP8X4), rhs_scale=scales[:], start=True, stop=True)
+
+        def gate(k):
+            b, cols = where(k)
+            zt[k] = work.tile([P, PACK, CH], BF16, name="z", tag="z")
+            for t in range(PACK):
+                nc.vector.scalar_tensor_tensor(out=zt[k][:, t, :], in0=ps1[k][t][:], scalar=bv_f[:, t:t + 1],
+                                               in1=rowb[:, b, cols], op0=ALU.add, op1=ALU.mult)
+
+        def relu_regroup(k):
+            gv[k] = work.tile([P, PACK * CH], BF16, name="gv", tag="gv", align_bytes=64)
+            nc.scalar.activation(out=grouped_view(gv[k][:]), in_=rows_view(zt[k][:]), func=ACT.Relu)
+
+        def quant_v(k):
+            nc.vector.quantize_mx(out=vq[:, k * CH:(k + 1) * CH].bitcast(FP8X4),
+                                  scales=vs[:, k * CH:(k + 1) * CH], in_=gv[k][:])
+
+        res = {}
+        st = {}
+
+        def unit(j, k):
+            b, cols = where(k)
+            h, half = divmod(k, HB // CH)
+            if half == 0:
+                res[(j, h)] = resp.tile([P, HB], F32, name="res", tag="res")
+            ps = psum.tile([P, CH], F32, name="ps2", tag="ps")
+            nc.tensor.matmul_mx(out=ps[:], lhsT=wq[1][:, j * P:(j + 1) * P].bitcast(FP8X4),
+                                lhsT_scale=ws[1][:, j * P:(j + 1) * P],
+                                rhs=vq[:, k * CH:(k + 1) * CH].bitcast(FP8X4),
+                                rhs_scale=vs[:, k * CH:(k + 1) * CH], start=True, stop=True)
+            nc.vector.scalar_tensor_tensor(out=res[(j, h)][:, half * CH:(half + 1) * CH], in0=ps[:],
+                                           scalar=negbo[:, j:j + 1], in1=x_sb[:, b, j, cols],
+                                           op0=ALU.max, op1=ALU.add, accum_out=sums[:, j, k:k + 1])
+
+        def squares(j, h, c0, c1, slot):
+            nc.scalar.activation(out=rowb[:, 0, c0:c1], in_=res[(j, h)][:, c0:c1], func=ACT.Square,
+                                 bias=minbo[:, j:j + 1], scale=1.0, accum_out=sqs[:, j, slot:slot + 1])
+
+        def small(j, name):
+            st[(j, name)] = stat.tile([P, 1], F32, name=name)
+            return st[(j, name)]
+
+        def stats_mean(j):
+            s1 = small(j, "s1")
+            nc.vector.tensor_reduce(out=s1[:], in_=sums[:, j, :], axis=AX.X, op=ALU.add)
+            nc.vector.tensor_scalar(out=small(j, "nmean")[:], in0=s1[:], scalar1=-1.0 / NT, scalar2=None,
+                                    op0=ALU.mult)
+            mc = small(j, "mc")
+            nc.vector.tensor_scalar(out=mc[:], in0=s1[:], scalar1=1.0 / NT, scalar2=minbo[:, j:j + 1],
+                                    op0=ALU.mult, op1=ALU.add)
+            nc.vector.tensor_tensor(out=small(j, "msq")[:], in0=mc[:], in1=mc[:], op=ALU.mult)
+
+        def stats_std(j, nslots):
+            s2 = small(j, "s2")
+            nc.vector.tensor_reduce(out=s2[:], in_=sqs[:, j, 0:nslots], axis=AX.X, op=ALU.add)
+            var = small(j, "var")
+            nc.vector.scalar_tensor_tensor(out=var[:], in0=s2[:], scalar=1.0 / NT, in1=st[(j, "msq")][:],
+                                           op0=ALU.mult, op1=ALU.subtract)
+            vare = small(j, "vare")
+            nc.vector.tensor_scalar(out=vare[:], in0=var[:], scalar1=0.0, scalar2=EPS, op0=ALU.max, op1=ALU.add)
+            nc.scalar.activation(out=small(j, "std")[:], in_=vare[:], func=ACT.Sqrt)
+
+        def stats_affine(j):
+            rstd = small(j, "rstd")
+            nc.vector.reciprocal(out=rstd[:], in_=st[(j, "std")][:])
+            sc = small(j, "sc")
+            nc.vector.tensor_tensor(out=sc[:], in0=ga_f[:, j:j + 1], in1=rstd[:], op=ALU.mult)
+            nc.vector.scalar_tensor_tensor(out=small(j, "sh")[:], in0=st[(j, "nmean")][:], scalar=sc[:, 0:1],
+                                           in1=be_f[:, j:j + 1], op0=ALU.mult, op1=ALU.add)
+
+        def norm_store(j, h, engine):
+            r = res[(j, h)]
+            sc = st[(j, "sc")]
+            sh = st[(j, "sh")]
+            if engine == "scalar":
+                nc.scalar.activation(out=r[:], in_=r[:], func=ACT.Identity, bias=sh[:, 0:1], scale=sc[:, 0:1])
+            elif engine == "vector":
+                nc.vector.tensor_scalar(out=r[:], in0=r[:], scalar1=sc[:, 0:1], scalar2=sh[:, 0:1],
+                                        op0=ALU.mult, op1=ALU.add)
+            else:
+                nc.gpsimd.tensor_scalar(out=r[:], in0=r[:], scalar1=sc[:, 0:1], scalar2=sh[:, 0:1],
+                                        op0=ALU.mult, op1=ALU.add)
+            b, half = divmod(h, N // HB)
+            nc.sync.dma_start(out=ov[b][:, j, half * HB:(half + 1) * HB], in_=r[:])
+
+        def after_unit(j, k):
+            last = j == PACK - 1
+            if j >= 1 and k == 3:
+                stats_mean(j - 1)
+                stats_std(j - 1, NHB)
+            if last and k >= NCHUNK - 2:
+                half = k - (NCHUNK - 2)
+                squares(j, NHB - 1, half * CH, (half + 1) * CH, NHB - 1 + half)
+            elif k % 2 == 1:
+                squares(j, k // 2, 0, HB, k // 2)
+            if j >= 1 and k == 5:
+                stats_affine(j - 1)
+                for h in range(NHB):
+                    norm_store(j - 1, h, "gpsimd")
+
+        w_transpose(0)
+        w_copy(0)
+        nc.vector.tensor_copy(out=bv_f[:], in_=bv_b[:])
+        w_quant(0)
+        for i in range(-2, NCHUNK + 1):
+            if i >= 1:
+                relu_regroup(i - 1)
+            if i + 2 < NCHUNK:
+                regroup_x(i + 2)
+            if 0 <= i + 1 < NCHUNK:
+                quant_x(i + 1)
+            if i == WO_AT:
+                w_transpose(1)
+            elif 0 <= i + 1 < NCHUNK:
+                matmul_1(i + 1)
+            if 0 <= i < NCHUNK:
+                gate(i)
+            if i == WO_AT:
+                matmul_1(i + 1)
+                w_copy(1)
+            if i == WO_AT + 2:
+                nc.vector.tensor_scalar(out=negbo[:], in0=bo_b[:], scalar1=-1.0, scalar2=None, op0=ALU.mult)
+                nc.vector.tensor_scalar(out=minbo[:], in0=bo_b[:], scalar1=0.0, scalar2=None, op0=ALU.min)
+                nc.vector.tensor_copy(out=ga_f[:], in_=ga_b[:])
+                nc.vector.tensor_copy(out=be_f[:], in_=be_b[:])
+            if i == NCHUNK:
+                for k in range(LEAD):
+                    unit(0, k)
+                    after_unit(0, k)
+            if i >= 1:
+                quant_v(i - 1)
+            if i == WO_AT:
+                w_quant(1)
+        for j in range(PACK):
+            for k in range(LEAD if j == 0 else 0, NCHUNK):
+                unit(j, k)
+                after_unit(j, k)
+        j = PACK - 1
+        stats_mean(j)
+        stats_std(j, NHB + 1)
+        stats_affine(j)
+        for h in range(NHB):
+            norm_store(j, h, ("vector", "scalar", "gpsimd")[h % 3])

@@ -26,7 +26,7 @@ EPS = 1e-5
 
 HB = 1024
 NHB = NT // HB
-X_ON_VECTOR = (1, 5, 9, 13)
+X_SCALAR = 384
 WO_AT = 2
 LEAD = 4
 
@@ -89,8 +89,8 @@ def tile_nonlocallayer_pa_t_kernel(tc, inputs, Wv, bv, row, Wo, bo, gamma, beta,
         load_vec(bv_b, bv)
         load_row(0, 0, CH)
         load_x(0, CH, 2 * CH)
-        load_x(0, 2 * CH, N)
         load_row(0, CH, N)
+        load_x(0, 2 * CH, N)
         load_w(1, Wo)
         load_vec(bo_b, bo)
         load_vec(ga_b, gamma)
@@ -137,12 +137,13 @@ def tile_nonlocallayer_pa_t_kernel(tc, inputs, Wv, bv, row, Wo, bo, gamma, beta,
             return src.rearrange("p t (c i) -> p c t i", i=4)
 
         def regroup_x(k):
-            b, cols = where(k)
+            b, q = divmod(k, QB)
+            c0 = q * CH
             gx[k] = work.tile([P, PACK * CH], BF16, name="gx", align_bytes=64)
-            if k in X_ON_VECTOR:
-                nc.vector.tensor_copy(out=grouped_view(gx[k][:]), in_=rows_view(x_sb[:, b, :, cols]))
-            else:
-                nc.scalar.copy(out=grouped_view(gx[k][:]), in_=rows_view(x_sb[:, b, :, cols]))
+            nc.scalar.copy(out=grouped_view(gx[k][:, 0:PACK * X_SCALAR]),
+                           in_=rows_view(x_sb[:, b, :, c0:c0 + X_SCALAR]))
+            nc.vector.tensor_copy(out=grouped_view(gx[k][:, PACK * X_SCALAR:PACK * CH]),
+                                  in_=rows_view(x_sb[:, b, :, c0 + X_SCALAR:c0 + CH]))
 
         def quant_x(k):
             codes = work.tile([P, CH], U32, name="xq", align_bytes=64)
@@ -256,7 +257,7 @@ def tile_nonlocallayer_pa_t_kernel(tc, inputs, Wv, bv, row, Wo, bo, gamma, beta,
             if j >= 1 and k == 5:
                 stats_affine(j - 1)
                 for h in range(NHB):
-                    norm_store(j - 1, h, "gpsimd")
+                    norm_store(j - 1, h, ("gpsimd", "scalar", "gpsimd", "vector")[h % 4])
 
         w_transpose(0)
         w_copy(0)

@@ -27,7 +27,7 @@ EPS = 1e-5
 HB = 1024
 NHB = NT // HB
 X_SCALAR = 384
-WO_AT = 2
+WO_AT = 12
 LEAD = 4
 
 
@@ -46,6 +46,8 @@ def tile_nonlocallayer_pa_t_kernel(tc, inputs, Wv, bv, row, Wo, bo, gamma, beta,
 
         x_sb = keep.tile([P, B, PACK, N], BF16, name="x_sb")
         rowb = keep.tile([P, B, N], BF16, name="rowb")
+        rsrc = keep.tile([P, N], BF16, name="rsrc")
+        sel = keep.tile([P, B, P], BF16, name="sel")
         vq = keep.tile([P, NT], U32, name="vq", align_bytes=64)
         vs = keep.tile([P, NT], U8, name="vs", align_bytes=64)
         wq = [keep.tile([P, 512], U32, name="wq%d" % s, align_bytes=64) for s in range(2)]
@@ -68,14 +70,15 @@ def tile_nonlocallayer_pa_t_kernel(tc, inputs, Wv, bv, row, Wo, bo, gamma, beta,
         nc.vector.memset(one[:], 1.0)
         nc.scalar.activation(out=one_s[:], in_=one[:], func=ACT.Sqrt)
         make_identity(nc, ident[:])
+        nc.vector.memset(rsrc[:], 0.0)
+        nc.vector.memset(sel[:], 0.0)
+        for b in range(B):
+            nc.vector.memset(sel[32 * b:32 * b + 1, b, :], 1.0)
 
         raw = [resp.tile([P, HB], F32, name="raw%d" % s, tag="res") for s in range(2)]
 
         def load_x(b, c0, c1):
             nc.sync.dma_start(out=x_sb[:, b, :, c0:c1], in_=xv[b][:, :, c0:c1])
-
-        def load_row(b, c0, c1):
-            nc.sync.dma_start(out=rowb[:, b, c0:c1], in_=row[b, c0:c1].partition_broadcast(P))
 
         def load_vec(dst, src):
             nc.sync.dma_start(out=dst[:], in_=src.rearrange("(p i) -> p i", i=PACK))
@@ -84,20 +87,18 @@ def tile_nonlocallayer_pa_t_kernel(tc, inputs, Wv, bv, row, Wo, bo, gamma, beta,
             nc.sync.dma_start(out=raw[s][:].bitcast(BF16).rearrange("p (i c) -> p i c", i=PACK),
                               in_=w.rearrange("(m i) c -> m i c", i=PACK))
 
+        nc.sync.dma_start(out=rsrc[0:P:32, :], in_=row)
         load_w(0, Wv)
         load_x(0, 0, CH)
         load_vec(bv_b, bv)
-        load_row(0, 0, CH)
         load_x(0, CH, 2 * CH)
-        load_row(0, CH, N)
         load_x(0, 2 * CH, N)
+        for b in range(1, B):
+            load_x(b, 0, N)
         load_w(1, Wo)
         load_vec(bo_b, bo)
         load_vec(ga_b, gamma)
         load_vec(be_b, beta)
-        for b in range(1, B):
-            load_x(b, 0, N)
-            load_row(b, 0, N)
 
         wps = {}
         wg = {}
@@ -119,6 +120,20 @@ def tile_nonlocallayer_pa_t_kernel(tc, inputs, Wv, bv, row, Wo, bo, gamma, beta,
 
         def w_quant(s):
             nc.vector.quantize_mx(out=wq[s][:].bitcast(FP8X4), scales=ws[s][:], in_=wg[s][:])
+
+        rps = {}
+
+        def spread_row(b):
+            for h in range(N // HB):
+                rps[(b, h)] = psum.tile([P, HB], BF16, name="rps", tag="ps")
+                for g in range(HB // CH):
+                    c0 = h * HB + g * CH
+                    nc.tensor.matmul(out=rps[(b, h)][:, g * CH:(g + 1) * CH], lhsT=sel[:, b, :],
+                                     rhs=rsrc[:, c0:c0 + CH], start=True, stop=True)
+
+        def copy_row(b):
+            for h in range(N // HB):
+                nc.vector.tensor_copy(out=rowb[:, b, h * HB:(h + 1) * HB], in_=rps[(b, h)][:])
 
         gx = {}
         xq = {}
@@ -260,6 +275,7 @@ def tile_nonlocallayer_pa_t_kernel(tc, inputs, Wv, bv, row, Wo, bo, gamma, beta,
                     norm_store(j - 1, h, ("gpsimd", "scalar", "gpsimd", "vector")[h % 4])
 
         w_transpose(0)
+        spread_row(0)
         w_copy(0)
         nc.vector.tensor_copy(out=bv_f[:], in_=bv_b[:])
         w_quant(0)
@@ -270,15 +286,24 @@ def tile_nonlocallayer_pa_t_kernel(tc, inputs, Wv, bv, row, Wo, bo, gamma, beta,
                 regroup_x(i + 2)
             if 0 <= i + 1 < NCHUNK:
                 quant_x(i + 1)
+            row_b = (i + 2) // QB if (i + 2) % QB == 0 and 0 < i + 2 < NCHUNK else 0
+            late = i == WO_AT or row_b > 0
             if i == WO_AT:
                 w_transpose(1)
-            elif 0 <= i + 1 < NCHUNK:
+            if row_b > 0:
+                spread_row(row_b)
+            if not late and 0 <= i + 1 < NCHUNK:
                 matmul_1(i + 1)
+            if i == -1:
+                copy_row(0)
             if 0 <= i < NCHUNK:
                 gate(i)
-            if i == WO_AT:
+            if late:
                 matmul_1(i + 1)
+            if i == WO_AT:
                 w_copy(1)
+            if row_b > 0:
+                copy_row(row_b)
             if i == WO_AT + 2:
                 nc.vector.tensor_scalar(out=negbo[:], in0=bo_b[:], scalar1=-1.0, scalar2=None, op0=ALU.mult)
                 nc.vector.tensor_scalar(out=minbo[:], in0=bo_b[:], scalar1=0.0, scalar2=None, op0=ALU.min)

@@ -9,6 +9,7 @@ BF16 = mybir.dt.bfloat16
 F32 = mybir.dt.float32
 U32 = mybir.dt.uint32
 U8 = mybir.dt.uint8
+I32 = mybir.dt.int32
 FP8X4 = mybir.dt.float8_e4m3fn_x4
 ALU = mybir.AluOpType
 ACT = mybir.ActivationFunctionType
@@ -26,7 +27,7 @@ EPS = 1e-5
 
 HB = 1024
 NHB = NT // HB
-X_SCALAR = 384
+X_SCALAR = 416
 WO_AT = 12
 LEAD = 4
 
@@ -39,7 +40,7 @@ def tile_nonlocallayer_pa_t_kernel(tc, inputs, Wv, bv, row, Wo, bo, gamma, beta,
     with ExitStack() as ctx:
         keep = ctx.enter_context(tc.tile_pool(name="keep", bufs=1))
         work = ctx.enter_context(tc.tile_pool(name="work", bufs=2))
-        resp = ctx.enter_context(tc.tile_pool(name="resp", bufs=17))
+        resp = ctx.enter_context(tc.tile_pool(name="resp", bufs=16))
         stat = ctx.enter_context(tc.tile_pool(name="stat", bufs=2))
         psum = ctx.enter_context(tc.psum_pool(name="psum", bufs=8))
         ctx.enter_context(tc.manual_schedule())
@@ -47,7 +48,7 @@ def tile_nonlocallayer_pa_t_kernel(tc, inputs, Wv, bv, row, Wo, bo, gamma, beta,
         x_sb = keep.tile([P, B, PACK, N], BF16, name="x_sb")
         rowb = keep.tile([P, B, N], BF16, name="rowb")
         rsrc = keep.tile([P, N], BF16, name="rsrc")
-        sel = keep.tile([P, B, P], BF16, name="sel")
+        sel = keep.tile([P, B * P], BF16, name="sel")
         vq = keep.tile([P, NT], U32, name="vq", align_bytes=64)
         vs = keep.tile([P, NT], U8, name="vs", align_bytes=64)
         wq = [keep.tile([P, 512], U32, name="wq%d" % s, align_bytes=64) for s in range(2)]
@@ -67,13 +68,13 @@ def tile_nonlocallayer_pa_t_kernel(tc, inputs, Wv, bv, row, Wo, bo, gamma, beta,
         one = keep.tile([P, 1], F32, name="one")
         one_s = keep.tile([P, 1], F32, name="one_s")
 
+        nc.vector.memset(rsrc[:].bitcast(I32), 0)
         nc.vector.memset(one[:], 1.0)
         nc.scalar.activation(out=one_s[:], in_=one[:], func=ACT.Sqrt)
         make_identity(nc, ident[:])
-        nc.vector.memset(rsrc[:], 0.0)
-        nc.vector.memset(sel[:], 0.0)
+        nc.vector.memset(sel[:].bitcast(I32), 0)
         for b in range(B):
-            nc.vector.memset(sel[32 * b:32 * b + 1, b, :], 1.0)
+            nc.vector.memset(sel[32 * b:32 * b + 1, b * P:(b + 1) * P], 1.0)
 
         raw = [resp.tile([P, HB], F32, name="raw%d" % s, tag="res") for s in range(2)]
 
@@ -87,9 +88,9 @@ def tile_nonlocallayer_pa_t_kernel(tc, inputs, Wv, bv, row, Wo, bo, gamma, beta,
             nc.sync.dma_start(out=raw[s][:].bitcast(BF16).rearrange("p (i c) -> p i c", i=PACK),
                               in_=w.rearrange("(m i) c -> m i c", i=PACK))
 
-        nc.sync.dma_start(out=rsrc[0:P:32, :], in_=row)
         load_w(0, Wv)
         load_x(0, 0, CH)
+        nc.sync.dma_start(out=rsrc[0:P:32, :], in_=row)
         load_vec(bv_b, bv)
         load_x(0, CH, 2 * CH)
         load_x(0, 2 * CH, N)
@@ -113,7 +114,7 @@ def tile_nonlocallayer_pa_t_kernel(tc, inputs, Wv, bv, row, Wo, bo, gamma, beta,
                         nc.tensor.transpose(wps[(s, h)][:, i2, u, :], words[:, 2 * h + i2, u, :], ident[:])
 
         def w_copy(s):
-            wg[s] = work.tile([P, PACK * 512], BF16, name="gw%d" % s, tag="gv", align_bytes=64)
+            wg[s] = work.tile([P, PACK * 512], BF16, name="gw%d" % s, tag="gv", bufs=3, align_bytes=64)
             g4 = wg[s][:].bitcast(F32).rearrange("p (h i m u) -> p h i m u", h=2, i=2, u=2)
             for h in range(2):
                 nc.vector.tensor_copy(out=g4[:, h], in_=wps[(s, h)].rearrange("p i u m -> p i m u"))
@@ -128,7 +129,7 @@ def tile_nonlocallayer_pa_t_kernel(tc, inputs, Wv, bv, row, Wo, bo, gamma, beta,
                 rps[(b, h)] = psum.tile([P, HB], BF16, name="rps", tag="ps")
                 for g in range(HB // CH):
                     c0 = h * HB + g * CH
-                    nc.tensor.matmul(out=rps[(b, h)][:, g * CH:(g + 1) * CH], lhsT=sel[:, b, :],
+                    nc.tensor.matmul(out=rps[(b, h)][:, g * CH:(g + 1) * CH], lhsT=sel[:, b * P:(b + 1) * P],
                                      rhs=rsrc[:, c0:c0 + CH], start=True, stop=True)
 
         def copy_row(b):
@@ -178,13 +179,13 @@ def tile_nonlocallayer_pa_t_kernel(tc, inputs, Wv, bv, row, Wo, bo, gamma, beta,
 
         def gate(k):
             b, cols = where(k)
-            zt[k] = work.tile([P, PACK, CH], BF16, name="z", tag="z")
+            zt[k] = work.tile([P, PACK, CH], BF16, name="z", tag="z", bufs=3)
             for t in range(PACK):
                 nc.vector.scalar_tensor_tensor(out=zt[k][:, t, :], in0=ps1[k][t][:], scalar=bv_f[:, t:t + 1],
                                                in1=rowb[:, b, cols], op0=ALU.add, op1=ALU.mult)
 
         def relu_regroup(k):
-            gv[k] = work.tile([P, PACK * CH], BF16, name="gv", tag="gv", align_bytes=64)
+            gv[k] = work.tile([P, PACK * CH], BF16, name="gv", tag="gv", bufs=3, align_bytes=64)
             nc.scalar.activation(out=grouped_view(gv[k][:]), in_=rows_view(zt[k][:]), func=ACT.Relu)
 
         def quant_v(k):
@@ -272,18 +273,14 @@ def tile_nonlocallayer_pa_t_kernel(tc, inputs, Wv, bv, row, Wo, bo, gamma, beta,
             if j >= 1 and k == 5:
                 stats_affine(j - 1)
                 for h in range(NHB):
-                    norm_store(j - 1, h, ("gpsimd", "scalar", "gpsimd", "vector")[h % 4])
+                    norm_store(j - 1, h, "gpsimd")
 
         w_transpose(0)
         spread_row(0)
         w_copy(0)
         nc.vector.tensor_copy(out=bv_f[:], in_=bv_b[:])
         w_quant(0)
-        for i in range(-2, NCHUNK + 1):
-            if i >= 1:
-                relu_regroup(i - 1)
-            if i + 2 < NCHUNK:
-                regroup_x(i + 2)
+        for i in range(-2, NCHUNK + 2):
             if 0 <= i + 1 < NCHUNK:
                 quant_x(i + 1)
             row_b = (i + 2) // QB if (i + 2) % QB == 0 and 0 < i + 2 < NCHUNK else 0
@@ -294,6 +291,10 @@ def tile_nonlocallayer_pa_t_kernel(tc, inputs, Wv, bv, row, Wo, bo, gamma, beta,
                 spread_row(row_b)
             if not late and 0 <= i + 1 < NCHUNK:
                 matmul_1(i + 1)
+            if i + 2 < NCHUNK:
+                regroup_x(i + 2)
+            if 1 <= i <= NCHUNK:
+                relu_regroup(i - 1)
             if i == -1:
                 copy_row(0)
             if 0 <= i < NCHUNK:
@@ -309,12 +310,12 @@ def tile_nonlocallayer_pa_t_kernel(tc, inputs, Wv, bv, row, Wo, bo, gamma, beta,
                 nc.vector.tensor_scalar(out=minbo[:], in0=bo_b[:], scalar1=0.0, scalar2=None, op0=ALU.min)
                 nc.vector.tensor_copy(out=ga_f[:], in_=ga_b[:])
                 nc.vector.tensor_copy(out=be_f[:], in_=be_b[:])
-            if i == NCHUNK:
+            if i == NCHUNK + 1:
                 for k in range(LEAD):
                     unit(0, k)
                     after_unit(0, k)
-            if i >= 1:
-                quant_v(i - 1)
+            if i >= 2:
+                quant_v(i - 2)
             if i == WO_AT:
                 w_quant(1)
         for j in range(PACK):

@@ -48,7 +48,7 @@ def tile_nonlocallayer_pa_t_kernel(tc, inputs, Wv, bv, row, Wo, bo, gamma, beta,
         x_sb = keep.tile([P, B, PACK, N], BF16, name="x_sb")
         rowb = keep.tile([P, B, N], BF16, name="rowb")
         rsrc = keep.tile([P, N], BF16, name="rsrc")
-        sel = keep.tile([P, B * P], BF16, name="sel")
+        ones = keep.tile([P, P], BF16, name="ones")
         vq = keep.tile([P, NT], U32, name="vq", align_bytes=64)
         vs = keep.tile([P, NT], U8, name="vs", align_bytes=64)
         wq = [keep.tile([P, 512], U32, name="wq%d" % s, align_bytes=64) for s in range(2)]
@@ -72,9 +72,7 @@ def tile_nonlocallayer_pa_t_kernel(tc, inputs, Wv, bv, row, Wo, bo, gamma, beta,
         nc.vector.memset(one[:], 1.0)
         nc.scalar.activation(out=one_s[:], in_=one[:], func=ACT.Sqrt)
         make_identity(nc, ident[:])
-        nc.vector.memset(sel[:].bitcast(I32), 0)
-        for b in range(B):
-            nc.vector.memset(sel[32 * b:32 * b + 1, b * P:(b + 1) * P], 1.0)
+        nc.vector.memset(ones[:], 1.0)
 
         raw = [resp.tile([P, HB], F32, name="raw%d" % s, tag="res") for s in range(2)]
 
@@ -90,12 +88,13 @@ def tile_nonlocallayer_pa_t_kernel(tc, inputs, Wv, bv, row, Wo, bo, gamma, beta,
 
         load_w(0, Wv)
         load_x(0, 0, CH)
-        nc.sync.dma_start(out=rsrc[0:P:32, :], in_=row)
+        nc.sync.dma_start(out=rsrc[0:1, :], in_=row[0:1, :])
         load_vec(bv_b, bv)
         load_x(0, CH, 2 * CH)
         load_x(0, 2 * CH, N)
         for b in range(1, B):
             load_x(b, 0, N)
+            nc.sync.dma_start(out=rowb[:, b, :], in_=row[b, :].partition_broadcast(P))
         load_w(1, Wo)
         load_vec(bo_b, bo)
         load_vec(ga_b, gamma)
@@ -124,17 +123,17 @@ def tile_nonlocallayer_pa_t_kernel(tc, inputs, Wv, bv, row, Wo, bo, gamma, beta,
 
         rps = {}
 
-        def spread_row(b):
+        def spread_row_0():
             for h in range(N // HB):
-                rps[(b, h)] = psum.tile([P, HB], BF16, name="rps", tag="ps")
+                rps[h] = psum.tile([P, HB], BF16, name="rps", tag="ps")
                 for g in range(HB // CH):
                     c0 = h * HB + g * CH
-                    nc.tensor.matmul(out=rps[(b, h)][:, g * CH:(g + 1) * CH], lhsT=sel[:, b * P:(b + 1) * P],
+                    nc.tensor.matmul(out=rps[h][:, g * CH:(g + 1) * CH], lhsT=ones[:],
                                      rhs=rsrc[:, c0:c0 + CH], start=True, stop=True)
 
-        def copy_row(b):
+        def copy_row_0():
             for h in range(N // HB):
-                nc.vector.tensor_copy(out=rowb[:, b, h * HB:(h + 1) * HB], in_=rps[(b, h)][:])
+                nc.vector.tensor_copy(out=rowb[:, 0, h * HB:(h + 1) * HB], in_=rps[h][:])
 
         gx = {}
         xq = {}
@@ -276,35 +275,28 @@ def tile_nonlocallayer_pa_t_kernel(tc, inputs, Wv, bv, row, Wo, bo, gamma, beta,
                     norm_store(j - 1, h, "gpsimd")
 
         w_transpose(0)
-        spread_row(0)
+        spread_row_0()
         w_copy(0)
         nc.vector.tensor_copy(out=bv_f[:], in_=bv_b[:])
         w_quant(0)
         for i in range(-2, NCHUNK + 2):
             if 0 <= i + 1 < NCHUNK:
                 quant_x(i + 1)
-            row_b = (i + 2) // QB if (i + 2) % QB == 0 and 0 < i + 2 < NCHUNK else 0
-            late = i == WO_AT or row_b > 0
             if i == WO_AT:
                 w_transpose(1)
-            if row_b > 0:
-                spread_row(row_b)
-            if not late and 0 <= i + 1 < NCHUNK:
+            elif 0 <= i + 1 < NCHUNK:
                 matmul_1(i + 1)
             if i + 2 < NCHUNK:
                 regroup_x(i + 2)
             if 1 <= i <= NCHUNK:
                 relu_regroup(i - 1)
             if i == -1:
-                copy_row(0)
+                copy_row_0()
             if 0 <= i < NCHUNK:
                 gate(i)
-            if late:
-                matmul_1(i + 1)
             if i == WO_AT:
+                matmul_1(i + 1)
                 w_copy(1)
-            if row_b > 0:
-                copy_row(row_b)
             if i == WO_AT + 2:
                 nc.vector.tensor_scalar(out=negbo[:], in0=bo_b[:], scalar1=-1.0, scalar2=None, op0=ALU.mult)
                 nc.vector.tensor_scalar(out=minbo[:], in0=bo_b[:], scalar1=0.0, scalar2=None, op0=ALU.min)

@@ -27,7 +27,7 @@ EPS = 1e-5
 
 HB = 1024
 NHB = NT // HB
-X_SCALAR = 416
+X_SCALAR = 352
 WO_AT = 12
 LEAD = 4
 

@@ -27,7 +27,7 @@ EPS = 1e-5
 
 HB = 1024
 NHB = NT // HB
-X_SCALAR = 352
+X_SCALAR = 320
 WO_AT = 12
 LEAD = 4
 
@@ -157,8 +157,9 @@ def tile_nonlocallayer_pa_t_kernel(tc, inputs, Wv, bv, row, Wo, bo, gamma, beta,
             gx[k] = work.tile([P, PACK * CH], BF16, name="gx", align_bytes=64)
             nc.scalar.copy(out=grouped_view(gx[k][:, 0:PACK * X_SCALAR]),
                            in_=rows_view(x_sb[:, b, :, c0:c0 + X_SCALAR]))
-            nc.vector.tensor_copy(out=grouped_view(gx[k][:, PACK * X_SCALAR:PACK * CH]),
-                                  in_=rows_view(x_sb[:, b, :, c0 + X_SCALAR:c0 + CH]))
+            nc.gpsimd.tensor_scalar(out=grouped_view(gx[k][:, PACK * X_SCALAR:PACK * CH]),
+                                    in0=rows_view(x_sb[:, b, :, c0 + X_SCALAR:c0 + CH]),
+                                    scalar1=1.0, scalar2=0.0, op0=ALU.mult, op1=ALU.add)
 
         def quant_x(k):
             codes = work.tile([P, CH], U32, name="xq", align_bytes=64)

@@ -45,7 +45,7 @@ def tile_nonlocallayer_pa_t_kernel(tc, inputs, Wv, bv, row, Wo, bo, gamma, beta,
         psum = ctx.enter_context(tc.psum_pool(name="psum", bufs=8))
         ctx.enter_context(tc.manual_schedule())
 
-        x_sb = keep.tile([P, B, PACK, N], BF16, name="x_sb")
+        x_sb = [keep.tile([P, PACK, CH], BF16, name="x%d" % k) for k in range(NCHUNK)]
         rowb = keep.tile([P, B, N], BF16, name="rowb")
         rsrc = keep.tile([P, N], BF16, name="rsrc")
         ones = keep.tile([P, P], BF16, name="ones")
@@ -69,6 +69,7 @@ def tile_nonlocallayer_pa_t_kernel(tc, inputs, Wv, bv, row, Wo, bo, gamma, beta,
         one_s = keep.tile([P, 1], F32, name="one_s")
 
         nc.vector.memset(rsrc[:].bitcast(I32), 0)
+        nc.scalar.dma_start(out=rsrc[0:1, :], in_=row[0:1, :])
         nc.vector.memset(one[:], 1.0)
         nc.scalar.activation(out=one_s[:], in_=one[:], func=ACT.Sqrt)
         make_identity(nc, ident[:])
@@ -76,8 +77,9 @@ def tile_nonlocallayer_pa_t_kernel(tc, inputs, Wv, bv, row, Wo, bo, gamma, beta,
 
         raw = [resp.tile([P, HB], F32, name="raw%d" % s, tag="res") for s in range(2)]
 
-        def load_x(b, c0, c1):
-            nc.sync.dma_start(out=x_sb[:, b, :, c0:c1], in_=xv[b][:, :, c0:c1])
+        def load_x(k):
+            b, q = divmod(k, QB)
+            nc.sync.dma_start(out=x_sb[k][:], in_=xv[b][:, :, q * CH:(q + 1) * CH])
 
         def load_vec(dst, src):
             nc.sync.dma_start(out=dst[:], in_=src.rearrange("(p i) -> p i", i=PACK))
@@ -87,13 +89,13 @@ def tile_nonlocallayer_pa_t_kernel(tc, inputs, Wv, bv, row, Wo, bo, gamma, beta,
                               in_=w.rearrange("(m i) c -> m i c", i=PACK))
 
         load_w(0, Wv)
-        load_x(0, 0, CH)
-        nc.sync.dma_start(out=rsrc[0:1, :], in_=row[0:1, :])
+        load_x(0)
         load_vec(bv_b, bv)
-        load_x(0, CH, 2 * CH)
-        load_x(0, 2 * CH, N)
+        for k in range(1, QB):
+            load_x(k)
         for b in range(1, B):
-            load_x(b, 0, N)
+            for q in range(QB):
+                load_x(b * QB + q)
             nc.sync.dma_start(out=rowb[:, b, :], in_=row[b, :].partition_broadcast(P))
         load_w(1, Wo)
         load_vec(bo_b, bo)
@@ -133,7 +135,7 @@ def tile_nonlocallayer_pa_t_kernel(tc, inputs, Wv, bv, row, Wo, bo, gamma, beta,
 
         def copy_row_0():
             for h in range(N // HB):
-                nc.vector.tensor_copy(out=rowb[:, 0, h * HB:(h + 1) * HB], in_=rps[h][:])
+                nc.scalar.copy(out=rowb[:, 0, h * HB:(h + 1) * HB], in_=rps[h][:])
 
         gx = {}
         xq = {}
@@ -152,13 +154,11 @@ def tile_nonlocallayer_pa_t_kernel(tc, inputs, Wv, bv, row, Wo, bo, gamma, beta,
             return src.rearrange("p t (c i) -> p c t i", i=4)
 
         def regroup_x(k):
-            b, q = divmod(k, QB)
-            c0 = q * CH
             gx[k] = work.tile([P, PACK * CH], BF16, name="gx", align_bytes=64)
             nc.scalar.copy(out=grouped_view(gx[k][:, 0:PACK * X_SCALAR]),
-                           in_=rows_view(x_sb[:, b, :, c0:c0 + X_SCALAR]))
+                           in_=rows_view(x_sb[k][:, :, 0:X_SCALAR]))
             nc.gpsimd.tensor_scalar(out=grouped_view(gx[k][:, PACK * X_SCALAR:PACK * CH]),
-                                    in0=rows_view(x_sb[:, b, :, c0 + X_SCALAR:c0 + CH]),
+                                    in0=rows_view(x_sb[k][:, :, X_SCALAR:CH]),
                                     scalar1=1.0, scalar2=0.0, op0=ALU.mult, op1=ALU.add)
 
         def quant_x(k):
@@ -196,7 +196,6 @@ def tile_nonlocallayer_pa_t_kernel(tc, inputs, Wv, bv, row, Wo, bo, gamma, beta,
         st = {}
 
         def unit(j, k):
-            b, cols = where(k)
             h, half = divmod(k, HB // CH)
             if half == 0:
                 res[(j, h)] = resp.tile([P, HB], F32, name="res", tag="res")
@@ -206,7 +205,7 @@ def tile_nonlocallayer_pa_t_kernel(tc, inputs, Wv, bv, row, Wo, bo, gamma, beta,
                                 rhs=vq[:, k * CH:(k + 1) * CH].bitcast(FP8X4),
                                 rhs_scale=vs[:, k * CH:(k + 1) * CH], start=True, stop=True)
             nc.vector.scalar_tensor_tensor(out=res[(j, h)][:, half * CH:(half + 1) * CH], in0=ps[:],
-                                           scalar=negbo[:, j:j + 1], in1=x_sb[:, b, j, cols],
+                                           scalar=negbo[:, j:j + 1], in1=x_sb[k][:, j, :],
                                            op0=ALU.max, op1=ALU.add, accum_out=sums[:, j, k:k + 1])
 
         def squares(j, h, c0, c1, slot):
@@ -275,12 +274,15 @@ def tile_nonlocallayer_pa_t_kernel(tc, inputs, Wv, bv, row, Wo, bo, gamma, beta,
                 for h in range(NHB):
                     norm_store(j - 1, h, "gpsimd")
 
-        w_transpose(0)
         spread_row_0()
+        copy_row_0()
+        w_transpose(0)
         w_copy(0)
-        nc.vector.tensor_copy(out=bv_f[:], in_=bv_b[:])
         w_quant(0)
+        nc.vector.tensor_copy(out=bv_f[:], in_=bv_b[:])
         for i in range(-2, NCHUNK + 2):
+            if i == 0:
+                gate(0)
             if 0 <= i + 1 < NCHUNK:
                 quant_x(i + 1)
             if i == WO_AT:
@@ -291,9 +293,7 @@ def tile_nonlocallayer_pa_t_kernel(tc, inputs, Wv, bv, row, Wo, bo, gamma, beta,
                 regroup_x(i + 2)
             if 1 <= i <= NCHUNK:
                 relu_regroup(i - 1)
-            if i == -1:
-                copy_row_0()
-            if 0 <= i < NCHUNK:
+            if 1 <= i < NCHUNK:
                 gate(i)
             if i == WO_AT:
                 matmul_1(i + 1)

@@ -47,7 +47,7 @@ def tile_nonlocallayer_pa_t_kernel(tc, inputs, Wv, bv, row, Wo, bo, gamma, beta,
 
         x_sb = [keep.tile([P, PACK, CH], BF16, name="x%d" % k) for k in range(NCHUNK)]
         rowb = keep.tile([P, B, N], BF16, name="rowb")
-        rsrc = keep.tile([P, N], BF16, name="rsrc")
+        rsrc = keep.tile([P, HB], BF16, name="rsrc")
         ones = keep.tile([P, P], BF16, name="ones")
         vq = keep.tile([P, NT], U32, name="vq", align_bytes=64)
         vs = keep.tile([P, NT], U8, name="vs", align_bytes=64)
@@ -69,7 +69,6 @@ def tile_nonlocallayer_pa_t_kernel(tc, inputs, Wv, bv, row, Wo, bo, gamma, beta,
         one_s = keep.tile([P, 1], F32, name="one_s")
 
         nc.vector.memset(rsrc[:].bitcast(I32), 0)
-        nc.scalar.dma_start(out=rsrc[0:1, :], in_=row[0:1, :])
         nc.vector.memset(one[:], 1.0)
         nc.scalar.activation(out=one_s[:], in_=one[:], func=ACT.Sqrt)
         make_identity(nc, ident[:])
@@ -90,9 +89,11 @@ def tile_nonlocallayer_pa_t_kernel(tc, inputs, Wv, bv, row, Wo, bo, gamma, beta,
 
         load_w(0, Wv)
         load_x(0)
+        nc.sync.dma_start(out=rsrc[0:1, :], in_=row[0:1, 0:HB])
         load_vec(bv_b, bv)
         for k in range(1, QB):
             load_x(k)
+        nc.sync.dma_start(out=rowb[:, 0, HB:N], in_=row[0, HB:N].partition_broadcast(P))
         for b in range(1, B):
             for q in range(QB):
                 load_x(b * QB + q)
@@ -123,19 +124,14 @@ def tile_nonlocallayer_pa_t_kernel(tc, inputs, Wv, bv, row, Wo, bo, gamma, beta,
         def w_quant(s):
             nc.vector.quantize_mx(out=wq[s][:].bitcast(FP8X4), scales=ws[s][:], in_=wg[s][:])
 
-        rps = {}
+        rps = psum.tile([P, HB], BF16, name="rps", tag="ps")
 
-        def spread_row_0():
-            for h in range(N // HB):
-                rps[h] = psum.tile([P, HB], BF16, name="rps", tag="ps")
-                for g in range(HB // CH):
-                    c0 = h * HB + g * CH
-                    nc.tensor.matmul(out=rps[h][:, g * CH:(g + 1) * CH], lhsT=ones[:],
-                                     rhs=rsrc[:, c0:c0 + CH], start=True, stop=True)
+        def spread_row():
+            for c0 in range(0, HB, CH):
+                nc.tensor.matmul(out=rps[:, c0:c0 + CH], lhsT=ones[:], rhs=rsrc[:, c0:c0 + CH], start=True, stop=True)
 
-        def copy_row_0():
-            for h in range(N // HB):
-                nc.scalar.copy(out=rowb[:, 0, h * HB:(h + 1) * HB], in_=rps[h][:])
+        def copy_row(engine_copy, k):
+            engine_copy(out=rowb[:, 0, k * CH:(k + 1) * CH], in_=rps[:, k * CH:(k + 1) * CH])
 
         gx = {}
         xq = {}
@@ -274,15 +270,16 @@ def tile_nonlocallayer_pa_t_kernel(tc, inputs, Wv, bv, row, Wo, bo, gamma, beta,
                 for h in range(NHB):
                     norm_store(j - 1, h, "gpsimd")
 
-        spread_row_0()
-        copy_row_0()
         w_transpose(0)
+        spread_row()
         w_copy(0)
         w_quant(0)
-        nc.vector.tensor_copy(out=bv_f[:], in_=bv_b[:])
         for i in range(-2, NCHUNK + 2):
             if i == 0:
+                nc.vector.tensor_copy(out=bv_f[:], in_=bv_b[:])
+                copy_row(nc.vector.tensor_copy, 0)
                 gate(0)
+                copy_row(nc.scalar.copy, 1)
             if 0 <= i + 1 < NCHUNK:
                 quant_x(i + 1)
             if i == WO_AT:

@@ -29,7 +29,7 @@ HB = 1024
 NHB = NT // HB
 X_SCALAR = 320
 WO_AT = 12
-LEAD = 4
+GROUP = 4
 
 
 def tile_nonlocallayer_pa_t_kernel(tc, inputs, Wv, bv, row, Wo, bo, gamma, beta, out):
@@ -70,7 +70,7 @@ def tile_nonlocallayer_pa_t_kernel(tc, inputs, Wv, bv, row, Wo, bo, gamma, beta,
 
         nc.vector.memset(rsrc[:].bitcast(I32), 0)
         nc.vector.memset(one[:], 1.0)
-        nc.scalar.activation(out=one_s[:], in_=one[:], func=ACT.Sqrt)
+        nc.scalar.activation(out=one_s[:], in_=one[:], func=ACT.Abs_reciprocal_sqrt)
         make_identity(nc, ident[:])
         nc.vector.memset(ones[:], 1.0)
 
@@ -176,7 +176,7 @@ def tile_nonlocallayer_pa_t_kernel(tc, inputs, Wv, bv, row, Wo, bo, gamma, beta,
         def gate(k):
             b, cols = where(k)
             zt[k] = work.tile([P, PACK, CH], BF16, name="z", tag="z", bufs=3)
-            for t in range(PACK):
+            for t in reversed(range(PACK)):
                 nc.vector.scalar_tensor_tensor(out=zt[k][:, t, :], in0=ps1[k][t][:], scalar=bv_f[:, t:t + 1],
                                                in1=rowb[:, b, cols], op0=ALU.add, op1=ALU.mult)
 
@@ -191,18 +191,22 @@ def tile_nonlocallayer_pa_t_kernel(tc, inputs, Wv, bv, row, Wo, bo, gamma, beta,
         res = {}
         st = {}
 
-        def unit(j, k):
-            h, half = divmod(k, HB // CH)
-            if half == 0:
-                res[(j, h)] = resp.tile([P, HB], F32, name="res", tag="res")
-            ps = psum.tile([P, CH], F32, name="ps2", tag="ps")
-            nc.tensor.matmul_mx(out=ps[:], lhsT=wq[1][:, j * P:(j + 1) * P].bitcast(FP8X4),
+        ps2 = {}
+
+        def matmul_2(j, k):
+            ps2[(j, k)] = psum.tile([P, CH], F32, name="ps2", tag="ps")
+            nc.tensor.matmul_mx(out=ps2[(j, k)][:], lhsT=wq[1][:, j * P:(j + 1) * P].bitcast(FP8X4),
                                 lhsT_scale=ws[1][:, j * P:(j + 1) * P],
                                 rhs=vq[:, k * CH:(k + 1) * CH].bitcast(FP8X4),
                                 rhs_scale=vs[:, k * CH:(k + 1) * CH], start=True, stop=True)
-            nc.vector.scalar_tensor_tensor(out=res[(j, h)][:, half * CH:(half + 1) * CH], in0=ps[:],
+
+        def join(j, k, n):
+            h, half = divmod(k, HB // CH)
+            if n % (HB // CH) == 0:
+                res[(j, h)] = resp.tile([P, HB], F32, name="res", tag="res")
+            nc.vector.scalar_tensor_tensor(out=res[(j, h)][:, half * CH:(half + 1) * CH], in0=ps2[(j, k)][:],
                                            scalar=negbo[:, j:j + 1], in1=x_sb[k][:, j, :],
-                                           op0=ALU.max, op1=ALU.add, accum_out=sums[:, j, k:k + 1])
+                                           op0=ALU.max, op1=ALU.add, accum_out=sums[:, j, n:n + 1])
 
         def squares(j, h, c0, c1, slot):
             nc.scalar.activation(out=rowb[:, 0, c0:c1], in_=res[(j, h)][:, c0:c1], func=ACT.Square,
@@ -212,33 +216,46 @@ def tile_nonlocallayer_pa_t_kernel(tc, inputs, Wv, bv, row, Wo, bo, gamma, beta,
             st[(j, name)] = stat.tile([P, 1], F32, name=name)
             return st[(j, name)]
 
-        def stats_mean(j):
-            s1 = small(j, "s1")
-            nc.vector.tensor_reduce(out=s1[:], in_=sums[:, j, :], axis=AX.X, op=ALU.add)
-            nc.vector.tensor_scalar(out=small(j, "nmean")[:], in0=s1[:], scalar1=-1.0 / NT, scalar2=None,
-                                    op0=ALU.mult)
+        def stats_mean(j, done):
+            last = NCHUNK - 1
+            if not done:
+                s1 = small(j, "s1")
+                nc.vector.tensor_reduce(out=s1[:], in_=sums[:, j, 0:last], axis=AX.X, op=ALU.add)
+                nc.vector.tensor_scalar(out=small(j, "mc_part")[:], in0=s1[:], scalar1=1.0 / NT,
+                                        scalar2=minbo[:, j:j + 1], op0=ALU.mult, op1=ALU.add)
+                return
             mc = small(j, "mc")
-            nc.vector.tensor_scalar(out=mc[:], in0=s1[:], scalar1=1.0 / NT, scalar2=minbo[:, j:j + 1],
-                                    op0=ALU.mult, op1=ALU.add)
+            nc.vector.tensor_scalar(out=mc[:], in0=sums[:, j, last:NCHUNK], scalar1=1.0 / NT,
+                                    scalar2=st[(j, "mc_part")][:], op0=ALU.mult, op1=ALU.add)
             nc.vector.tensor_tensor(out=small(j, "msq")[:], in0=mc[:], in1=mc[:], op=ALU.mult)
 
-        def stats_std(j, nslots):
+        def stats_square(j, nslots):
             s2 = small(j, "s2")
-            nc.vector.tensor_reduce(out=s2[:], in_=sqs[:, j, 0:nslots], axis=AX.X, op=ALU.add)
-            var = small(j, "var")
-            nc.vector.scalar_tensor_tensor(out=var[:], in0=s2[:], scalar=1.0 / NT, in1=st[(j, "msq")][:],
-                                           op0=ALU.mult, op1=ALU.subtract)
-            vare = small(j, "vare")
-            nc.vector.tensor_scalar(out=vare[:], in0=var[:], scalar1=0.0, scalar2=EPS, op0=ALU.max, op1=ALU.add)
-            nc.scalar.activation(out=small(j, "std")[:], in_=vare[:], func=ACT.Sqrt)
+            nc.vector.tensor_reduce(out=s2[:], in_=sqs[:, j, 0:nslots - 1], axis=AX.X, op=ALU.add)
+            nc.vector.tensor_scalar(out=small(j, "sq_part")[:], in0=s2[:], scalar1=1.0 / NT, scalar2=None,
+                                    op0=ALU.mult)
 
-        def stats_affine(j):
+        def stats_base(j):
+            nc.vector.scalar_tensor_tensor(out=small(j, "base")[:], in0=st[(j, "sq_part")][:], scalar=EPS,
+                                           in1=st[(j, "msq")][:], op0=ALU.add, op1=ALU.subtract)
+            nc.vector.scalar_tensor_tensor(out=small(j, "ngm")[:], in0=minbo[:, j:j + 1], scalar=st[(j, "mc")][:],
+                                           in1=ga_f[:, j:j + 1], op0=ALU.subtract, op1=ALU.mult)
+
+        def stats_affine(j, nslots):
             rstd = small(j, "rstd")
-            nc.vector.reciprocal(out=rstd[:], in_=st[(j, "std")][:])
+            nc.scalar.activation(out=rstd[:], in_=sqs[:, j, nslots - 1:nslots], func=ACT.Abs_reciprocal_sqrt,
+                                 bias=st[(j, "base")][:], scale=1.0 / NT)
             sc = small(j, "sc")
-            nc.vector.tensor_tensor(out=sc[:], in0=ga_f[:, j:j + 1], in1=rstd[:], op=ALU.mult)
-            nc.vector.scalar_tensor_tensor(out=small(j, "sh")[:], in0=st[(j, "nmean")][:], scalar=sc[:, 0:1],
-                                           in1=be_f[:, j:j + 1], op0=ALU.mult, op1=ALU.add)
+            sh = small(j, "sh")
+            if j == PACK - 1:
+                nc.vector.tensor_scalar(out=sc[:], in0=rstd[:], scalar1=ga_f[:, j:j + 1], scalar2=None, op0=ALU.mult)
+                nc.scalar.activation(out=sh[:], in_=rstd[:], func=ACT.Identity, bias=be_f[:, j:j + 1],
+                                     scale=st[(j, "ngm")][:])
+            else:
+                nc.gpsimd.tensor_scalar(out=sc[:], in0=rstd[:], scalar1=ga_f[:, j:j + 1], scalar2=0.0,
+                                        op0=ALU.mult, op1=ALU.add)
+                nc.gpsimd.tensor_scalar(out=sh[:], in0=rstd[:], scalar1=st[(j, "ngm")][:], scalar2=be_f[:, j:j + 1],
+                                        op0=ALU.mult, op1=ALU.add)
 
         def norm_store(j, h, engine):
             r = res[(j, h)]
@@ -255,20 +272,43 @@ def tile_nonlocallayer_pa_t_kernel(tc, inputs, Wv, bv, row, Wo, bo, gamma, beta,
             b, half = divmod(h, N // HB)
             nc.sync.dma_start(out=ov[b][:, j, half * HB:(half + 1) * HB], in_=r[:])
 
-        def after_unit(j, k):
-            last = j == PACK - 1
-            if j >= 1 and k == 3:
-                stats_mean(j - 1)
-                stats_std(j - 1, NHB)
-            if last and k >= NCHUNK - 2:
-                half = k - (NCHUNK - 2)
-                squares(j, NHB - 1, half * CH, (half + 1) * CH, NHB - 1 + half)
-            elif k % 2 == 1:
-                squares(j, k // 2, 0, HB, k // 2)
-            if j >= 1 and k == 5:
-                stats_affine(j - 1)
-                for h in range(NHB):
+        def finish_stats(j):
+            nslots = NHB + 1 if j == PACK - 1 else NHB
+            stats_square(j, nslots)
+            stats_base(j)
+            stats_affine(j, nslots)
+
+        chunk_order = [g0 + GROUP - 1 - i for g0 in range(0, NCHUNK, GROUP) for i in range(GROUP)]
+        tile_order = [chunk_order[n] * CH // HB for n in range(0, NCHUNK, HB // CH)]
+
+        def after_join(j, k, n):
+            h, half = divmod(k, HB // CH)
+            if n == NCHUNK - 1:
+                stats_mean(j, True)
+            if j == PACK - 1 and n == NCHUNK - 1:
+                norm_store(j - 1, tile_order[NHB - 1], "vector")
+            if j == PACK - 1 and n >= NCHUNK - 2:
+                squares(j, h, half * CH, (half + 1) * CH, n - NHB + 1)
+            elif n % 2 == 1:
+                squares(j, h, 0, HB, n // 2)
+            if n == NCHUNK - 2:
+                stats_mean(j, False)
+            if j == PACK - 1 and n == NCHUNK - 1:
+                finish_stats(j)
+            if j >= 1 and n == 0:
+                finish_stats(j - 1)
+                for h in tile_order[0:NHB - 1]:
                     norm_store(j - 1, h, "gpsimd")
+                if j < PACK - 1:
+                    norm_store(j - 1, tile_order[NHB - 1], "gpsimd")
+
+        def stage_2(j, g):
+            ks = chunk_order[g * GROUP:(g + 1) * GROUP]
+            for k in reversed(ks):
+                matmul_2(j, k)
+            for i, k in enumerate(ks):
+                join(j, k, g * GROUP + i)
+                after_join(j, k, g * GROUP + i)
 
         w_transpose(0)
         spread_row()
@@ -301,20 +341,13 @@ def tile_nonlocallayer_pa_t_kernel(tc, inputs, Wv, bv, row, Wo, bo, gamma, beta,
                 nc.vector.tensor_copy(out=ga_f[:], in_=ga_b[:])
                 nc.vector.tensor_copy(out=be_f[:], in_=be_b[:])
             if i == NCHUNK + 1:
-                for k in range(LEAD):
-                    unit(0, k)
-                    after_unit(0, k)
+                stage_2(0, 0)
             if i >= 2:
                 quant_v(i - 2)
             if i == WO_AT:
                 w_quant(1)
         for j in range(PACK):
-            for k in range(LEAD if j == 0 else 0, NCHUNK):
-                unit(j, k)
-                after_unit(j, k)
-        j = PACK - 1
-        stats_mean(j)
-        stats_std(j, NHB + 1)
-        stats_affine(j)
-        for h in range(NHB):
-            norm_store(j, h, ("vector", "scalar", "gpsimd")[h % 3])
+            for g in range(1 if j == 0 else 0, NCHUNK // GROUP):
+                stage_2(j, g)
+        for i, h in enumerate(tile_order):
+            norm_store(PACK - 1, h, ("vector", "scalar", "gpsimd")[i % 3])

@@ -62,9 +62,10 @@ def tile_nonlocallayer_pa_t_kernel(tc, inputs, Wv, bv, row, Wo, bo, gamma, beta,
         negbo = keep.tile([P, PACK], F32, name="negbo")
         minbo = keep.tile([P, PACK], F32, name="minbo")
         ga_f = keep.tile([P, PACK], F32, name="ga_f")
+        ga_n = keep.tile([P, PACK], F32, name="ga_n")
         be_f = keep.tile([P, PACK], F32, name="be_f")
-        sums = keep.tile([P, PACK, NCHUNK], F32, name="sums")
-        sqs = keep.tile([P, PACK, NHB + 1], F32, name="sqs")
+        sums = keep.tile([P, PACK, 1 + NCHUNK], F32, name="sums")
+        sqs = keep.tile([P, PACK, 1 + NHB + 1], F32, name="sqs")
         one = keep.tile([P, 1], F32, name="one")
         one_s = keep.tile([P, 1], F32, name="one_s")
 
@@ -176,7 +177,7 @@ def tile_nonlocallayer_pa_t_kernel(tc, inputs, Wv, bv, row, Wo, bo, gamma, beta,
         def gate(k):
             b, cols = where(k)
             zt[k] = work.tile([P, PACK, CH], BF16, name="z", tag="z", bufs=3)
-            for t in reversed(range(PACK)):
+            for t in range(PACK) if k < 2 else reversed(range(PACK)):
                 nc.vector.scalar_tensor_tensor(out=zt[k][:, t, :], in0=ps1[k][t][:], scalar=bv_f[:, t:t + 1],
                                                in1=rowb[:, b, cols], op0=ALU.add, op1=ALU.mult)
 
@@ -206,55 +207,51 @@ def tile_nonlocallayer_pa_t_kernel(tc, inputs, Wv, bv, row, Wo, bo, gamma, beta,
                 res[(j, h)] = resp.tile([P, HB], F32, name="res", tag="res")
             nc.vector.scalar_tensor_tensor(out=res[(j, h)][:, half * CH:(half + 1) * CH], in0=ps2[(j, k)][:],
                                            scalar=negbo[:, j:j + 1], in1=x_sb[k][:, j, :],
-                                           op0=ALU.max, op1=ALU.add, accum_out=sums[:, j, n:n + 1])
+                                           op0=ALU.max, op1=ALU.add, accum_out=sums[:, j, 1 + n:2 + n])
 
         def squares(j, h, c0, c1, slot):
             nc.scalar.activation(out=rowb[:, 0, c0:c1], in_=res[(j, h)][:, c0:c1], func=ACT.Square,
-                                 bias=minbo[:, j:j + 1], scale=1.0, accum_out=sqs[:, j, slot:slot + 1])
+                                 bias=minbo[:, j:j + 1], scale=1.0, accum_out=sqs[:, j, 1 + slot:2 + slot])
 
         def small(j, name):
             st[(j, name)] = stat.tile([P, 1], F32, name=name)
             return st[(j, name)]
 
-        def stats_mean(j, done):
-            last = NCHUNK - 1
-            if not done:
-                s1 = small(j, "s1")
-                nc.vector.tensor_reduce(out=s1[:], in_=sums[:, j, 0:last], axis=AX.X, op=ALU.add)
-                nc.vector.tensor_scalar(out=small(j, "mc_part")[:], in0=s1[:], scalar1=1.0 / NT,
-                                        scalar2=minbo[:, j:j + 1], op0=ALU.mult, op1=ALU.add)
-                return
-            mc = small(j, "mc")
-            nc.vector.tensor_scalar(out=mc[:], in0=sums[:, j, last:NCHUNK], scalar1=1.0 / NT,
-                                    scalar2=st[(j, "mc_part")][:], op0=ALU.mult, op1=ALU.add)
-            nc.vector.tensor_tensor(out=small(j, "msq")[:], in0=mc[:], in1=mc[:], op=ALU.mult)
+        def stats_sum(j):
+            nc.vector.tensor_reduce(out=small(j, "s1_part")[:], in_=sums[:, j, 0:NCHUNK - 1], axis=AX.X, op=ALU.add)
 
-        def stats_square(j, nslots):
-            s2 = small(j, "s2")
-            nc.vector.tensor_reduce(out=s2[:], in_=sqs[:, j, 0:nslots - 1], axis=AX.X, op=ALU.add)
-            nc.vector.tensor_scalar(out=small(j, "sq_part")[:], in0=s2[:], scalar1=1.0 / NT, scalar2=None,
-                                    op0=ALU.mult)
+        def stats_total(j):
+            nc.vector.tensor_reduce(out=small(j, "s2_part")[:], in_=sqs[:, j, 0:NHB], axis=AX.X, op=ALU.add)
+            nc.vector.scalar_tensor_tensor(out=small(j, "s1")[:], in0=sums[:, j, NCHUNK:NCHUNK + 1],
+                                           scalar=sums[:, j, NCHUNK - 1:NCHUNK], in1=st[(j, "s1_part")][:],
+                                           op0=ALU.add, op1=ALU.add)
 
-        def stats_base(j):
-            nc.vector.scalar_tensor_tensor(out=small(j, "base")[:], in0=st[(j, "sq_part")][:], scalar=EPS,
-                                           in1=st[(j, "msq")][:], op0=ALU.add, op1=ALU.subtract)
-            nc.vector.scalar_tensor_tensor(out=small(j, "ngm")[:], in0=minbo[:, j:j + 1], scalar=st[(j, "mc")][:],
+        def stats_square(j):
+            nc.vector.tensor_scalar(out=small(j, "s2_n")[:], in0=sqs[:, j, NHB:NHB + 1], scalar1=st[(j, "s2_part")][:],
+                                    scalar2=float(NT), op0=ALU.add, op1=ALU.mult)
+
+        def stats_mean(j):
+            nc.vector.scalar_tensor_tensor(out=small(j, "mean_n")[:], in0=sums[:, j, 0:1], scalar=st[(j, "s1")][:],
                                            in1=ga_f[:, j:j + 1], op0=ALU.subtract, op1=ALU.mult)
 
-        def stats_affine(j, nslots):
+        def stats_base(j):
+            nc.vector.scalar_tensor_tensor(out=small(j, "base")[:], in0=st[(j, "s1")][:], scalar=st[(j, "s1")][:],
+                                           in1=st[(j, "s2_n")][:], op0=ALU.mult, op1=ALU.subtract)
+
+        def stats_affine(j):
             rstd = small(j, "rstd")
-            nc.scalar.activation(out=rstd[:], in_=sqs[:, j, nslots - 1:nslots], func=ACT.Abs_reciprocal_sqrt,
-                                 bias=st[(j, "base")][:], scale=1.0 / NT)
+            nc.scalar.activation(out=rstd[:], in_=sqs[:, j, NHB + 1:NHB + 2], func=ACT.Abs_reciprocal_sqrt,
+                                 bias=st[(j, "base")][:], scale=-float(NT))
             sc = small(j, "sc")
             sh = small(j, "sh")
             if j == PACK - 1:
-                nc.vector.tensor_scalar(out=sc[:], in0=rstd[:], scalar1=ga_f[:, j:j + 1], scalar2=None, op0=ALU.mult)
+                nc.vector.tensor_scalar(out=sc[:], in0=rstd[:], scalar1=ga_n[:, j:j + 1], scalar2=None, op0=ALU.mult)
                 nc.scalar.activation(out=sh[:], in_=rstd[:], func=ACT.Identity, bias=be_f[:, j:j + 1],
-                                     scale=st[(j, "ngm")][:])
+                                     scale=st[(j, "mean_n")][:])
             else:
-                nc.gpsimd.tensor_scalar(out=sc[:], in0=rstd[:], scalar1=ga_f[:, j:j + 1], scalar2=0.0,
+                nc.gpsimd.tensor_scalar(out=sc[:], in0=rstd[:], scalar1=ga_n[:, j:j + 1], scalar2=0.0,
                                         op0=ALU.mult, op1=ALU.add)
-                nc.gpsimd.tensor_scalar(out=sh[:], in0=rstd[:], scalar1=st[(j, "ngm")][:], scalar2=be_f[:, j:j + 1],
+                nc.gpsimd.tensor_scalar(out=sh[:], in0=rstd[:], scalar1=st[(j, "mean_n")][:], scalar2=be_f[:, j:j + 1],
                                         op0=ALU.mult, op1=ALU.add)
 
         def norm_store(j, h, engine):
@@ -272,35 +269,27 @@ def tile_nonlocallayer_pa_t_kernel(tc, inputs, Wv, bv, row, Wo, bo, gamma, beta,
             b, half = divmod(h, N // HB)
             nc.sync.dma_start(out=ov[b][:, j, half * HB:(half + 1) * HB], in_=r[:])
 
-        def finish_stats(j):
-            nslots = NHB + 1 if j == PACK - 1 else NHB
-            stats_square(j, nslots)
-            stats_base(j)
-            stats_affine(j, nslots)
-
         chunk_order = [g0 + GROUP - 1 - i for g0 in range(0, NCHUNK, GROUP) for i in range(GROUP)]
         tile_order = [chunk_order[n] * CH // HB for n in range(0, NCHUNK, HB // CH)]
 
         def after_join(j, k, n):
             h, half = divmod(k, HB // CH)
-            if n == NCHUNK - 1:
-                stats_mean(j, True)
-            if j == PACK - 1 and n == NCHUNK - 1:
-                norm_store(j - 1, tile_order[NHB - 1], "vector")
-            if j == PACK - 1 and n >= NCHUNK - 2:
+            if n >= NCHUNK - 2:
                 squares(j, h, half * CH, (half + 1) * CH, n - NHB + 1)
             elif n % 2 == 1:
                 squares(j, h, 0, HB, n // 2)
             if n == NCHUNK - 2:
-                stats_mean(j, False)
-            if j == PACK - 1 and n == NCHUNK - 1:
-                finish_stats(j)
+                stats_sum(j)
             if j >= 1 and n == 0:
-                finish_stats(j - 1)
-                for h in tile_order[0:NHB - 1]:
-                    norm_store(j - 1, h, "gpsimd")
-                if j < PACK - 1:
-                    norm_store(j - 1, tile_order[NHB - 1], "gpsimd")
+                stats_total(j - 1)
+            if j >= 1 and n == 1:
+                stats_square(j - 1)
+                stats_mean(j - 1)
+            if j >= 1 and n == 2:
+                stats_base(j - 1)
+                stats_affine(j - 1)
+                for tile in tile_order:
+                    norm_store(j - 1, tile, "gpsimd")
 
         def stage_2(j, g):
             ks = chunk_order[g * GROUP:(g + 1) * GROUP]
@@ -336,10 +325,17 @@ def tile_nonlocallayer_pa_t_kernel(tc, inputs, Wv, bv, row, Wo, bo, gamma, beta,
                 matmul_1(i + 1)
                 w_copy(1)
             if i == WO_AT + 2:
-                nc.vector.tensor_scalar(out=negbo[:], in0=bo_b[:], scalar1=-1.0, scalar2=None, op0=ALU.mult)
-                nc.vector.tensor_scalar(out=minbo[:], in0=bo_b[:], scalar1=0.0, scalar2=None, op0=ALU.min)
-                nc.vector.tensor_copy(out=ga_f[:], in_=ga_b[:])
-                nc.vector.tensor_copy(out=be_f[:], in_=be_b[:])
+                nc.gpsimd.tensor_scalar(out=negbo[:], in0=bo_b[:], scalar1=-1.0, scalar2=0.0, op0=ALU.mult, op1=ALU.add)
+                nc.gpsimd.tensor_scalar(out=minbo[:], in0=bo_b[:], scalar1=0.0, scalar2=0.0, op0=ALU.min, op1=ALU.add)
+                nc.gpsimd.tensor_scalar(out=ga_f[:], in0=ga_b[:], scalar1=1.0, scalar2=0.0, op0=ALU.mult, op1=ALU.add)
+                nc.gpsimd.tensor_scalar(out=ga_n[:], in0=ga_b[:], scalar1=float(NT), scalar2=0.0,
+                                        op0=ALU.mult, op1=ALU.add)
+                nc.gpsimd.tensor_scalar(out=be_f[:], in0=be_b[:], scalar1=1.0, scalar2=0.0, op0=ALU.mult, op1=ALU.add)
+            if i == WO_AT + 3:
+                for j in range(PACK):
+                    nc.vector.tensor_scalar(out=sums[:, j, 0:1], in0=minbo[:, j:j + 1], scalar1=float(NT), scalar2=None,
+                                            op0=ALU.mult)
+                    nc.vector.tensor_scalar(out=sqs[:, j, 0:1], in0=one[:], scalar1=NT * EPS, scalar2=None, op0=ALU.mult)
             if i == NCHUNK + 1:
                 stage_2(0, 0)
             if i >= 2:
@@ -349,5 +345,11 @@ def tile_nonlocallayer_pa_t_kernel(tc, inputs, Wv, bv, row, Wo, bo, gamma, beta,
         for j in range(PACK):
             for g in range(1 if j == 0 else 0, NCHUNK // GROUP):
                 stage_2(j, g)
+        j = PACK - 1
+        stats_total(j)
+        stats_square(j)
+        stats_base(j)
+        stats_mean(j)
+        stats_affine(j)
         for i, h in enumerate(tile_order):
-            norm_store(PACK - 1, h, ("vector", "scalar", "gpsimd")[i % 3])
+            norm_store(j, h, ("vector", "scalar", "gpsimd")[i % 3])

@@ -29,6 +29,8 @@ HB = 1024
 NHB = NT // HB
 X_SCALAR = 320
 WO_AT = 12
+G_NORM = (7, 7, 6)
+S_NORM_AT = 5
 GROUP = 4
 
 
@@ -72,6 +74,8 @@ def tile_nonlocallayer_pa_t_kernel(tc, inputs, Wv, bv, row, Wo, bo, gamma, beta,
         nc.vector.memset(rsrc[:].bitcast(I32), 0)
         nc.vector.memset(one[:], 1.0)
         nc.scalar.activation(out=one_s[:], in_=one[:], func=ACT.Abs_reciprocal_sqrt)
+        for j in range(PACK):
+            nc.vector.tensor_scalar(out=sqs[:, j, 0:1], in0=one[:], scalar1=NT * EPS, scalar2=None, op0=ALU.mult)
         make_identity(nc, ident[:])
         nc.vector.memset(ones[:], 1.0)
 
@@ -242,17 +246,18 @@ def tile_nonlocallayer_pa_t_kernel(tc, inputs, Wv, bv, row, Wo, bo, gamma, beta,
             rstd = small(j, "rstd")
             nc.scalar.activation(out=rstd[:], in_=sqs[:, j, NHB + 1:NHB + 2], func=ACT.Abs_reciprocal_sqrt,
                                  bias=st[(j, "base")][:], scale=-float(NT))
-            sc = small(j, "sc")
-            sh = small(j, "sh")
             if j == PACK - 1:
-                nc.vector.tensor_scalar(out=sc[:], in0=rstd[:], scalar1=ga_n[:, j:j + 1], scalar2=None, op0=ALU.mult)
-                nc.scalar.activation(out=sh[:], in_=rstd[:], func=ACT.Identity, bias=be_f[:, j:j + 1],
+                nc.scalar.activation(out=small(j, "sh")[:], in_=rstd[:], func=ACT.Identity, bias=be_f[:, j:j + 1],
                                      scale=st[(j, "mean_n")][:])
             else:
-                nc.gpsimd.tensor_scalar(out=sc[:], in0=rstd[:], scalar1=ga_n[:, j:j + 1], scalar2=0.0,
+                nc.gpsimd.tensor_scalar(out=small(j, "sc")[:], in0=rstd[:], scalar1=ga_n[:, j:j + 1], scalar2=0.0,
                                         op0=ALU.mult, op1=ALU.add)
-                nc.gpsimd.tensor_scalar(out=sh[:], in0=rstd[:], scalar1=st[(j, "mean_n")][:], scalar2=be_f[:, j:j + 1],
-                                        op0=ALU.mult, op1=ALU.add)
+                nc.gpsimd.tensor_scalar(out=small(j, "sh")[:], in0=rstd[:], scalar1=st[(j, "mean_n")][:],
+                                        scalar2=be_f[:, j:j + 1], op0=ALU.mult, op1=ALU.add)
+
+        def stats_scale(j):
+            nc.vector.tensor_scalar(out=small(j, "sc")[:], in0=st[(j, "rstd")][:], scalar1=ga_n[:, j:j + 1],
+                                    scalar2=None, op0=ALU.mult)
 
         def norm_store(j, h, engine):
             r = res[(j, h)]
@@ -269,10 +274,23 @@ def tile_nonlocallayer_pa_t_kernel(tc, inputs, Wv, bv, row, Wo, bo, gamma, beta,
             b, half = divmod(h, N // HB)
             nc.sync.dma_start(out=ov[b][:, j, half * HB:(half + 1) * HB], in_=r[:])
 
+        def finish_stats(j):
+            stats_total(j)
+            stats_square(j)
+            stats_mean(j)
+            stats_base(j)
+            stats_affine(j)
+
         chunk_order = [g0 + GROUP - 1 - i for g0 in range(0, NCHUNK, GROUP) for i in range(GROUP)]
         tile_order = [chunk_order[n] * CH // HB for n in range(0, NCHUNK, HB // CH)]
 
         def after_join(j, k, n):
+            if j >= 1 and n == 1:
+                finish_stats(j - 1)
+                for tile in tile_order[0:G_NORM[j - 1]]:
+                    norm_store(j - 1, tile, "gpsimd")
+            if 1 <= j < PACK - 1 and n == S_NORM_AT:
+                norm_store(j - 1, tile_order[NHB - 1], "scalar")
             h, half = divmod(k, HB // CH)
             if n >= NCHUNK - 2:
                 squares(j, h, half * CH, (half + 1) * CH, n - NHB + 1)
@@ -280,16 +298,6 @@ def tile_nonlocallayer_pa_t_kernel(tc, inputs, Wv, bv, row, Wo, bo, gamma, beta,
                 squares(j, h, 0, HB, n // 2)
             if n == NCHUNK - 2:
                 stats_sum(j)
-            if j >= 1 and n == 0:
-                stats_total(j - 1)
-            if j >= 1 and n == 1:
-                stats_square(j - 1)
-                stats_mean(j - 1)
-            if j >= 1 and n == 2:
-                stats_base(j - 1)
-                stats_affine(j - 1)
-                for tile in tile_order:
-                    norm_store(j - 1, tile, "gpsimd")
 
         def stage_2(j, g):
             ks = chunk_order[g * GROUP:(g + 1) * GROUP]
@@ -332,10 +340,7 @@ def tile_nonlocallayer_pa_t_kernel(tc, inputs, Wv, bv, row, Wo, bo, gamma, beta,
                                         op0=ALU.mult, op1=ALU.add)
                 nc.gpsimd.tensor_scalar(out=be_f[:], in0=be_b[:], scalar1=1.0, scalar2=0.0, op0=ALU.mult, op1=ALU.add)
             if i == WO_AT + 3:
-                for j in range(PACK):
-                    nc.vector.tensor_scalar(out=sums[:, j, 0:1], in0=minbo[:, j:j + 1], scalar1=float(NT), scalar2=None,
-                                            op0=ALU.mult)
-                    nc.vector.tensor_scalar(out=sqs[:, j, 0:1], in0=one[:], scalar1=NT * EPS, scalar2=None, op0=ALU.mult)
+                nc.scalar.activation(out=sums[:, :, 0:1], in_=minbo[:].unsqueeze(2), func=ACT.Copy, scale=float(NT))
             if i == NCHUNK + 1:
                 stage_2(0, 0)
             if i >= 2:
@@ -346,10 +351,10 @@ def tile_nonlocallayer_pa_t_kernel(tc, inputs, Wv, bv, row, Wo, bo, gamma, beta,
             for g in range(1 if j == 0 else 0, NCHUNK // GROUP):
                 stage_2(j, g)
         j = PACK - 1
-        stats_total(j)
-        stats_square(j)
-        stats_base(j)
-        stats_mean(j)
-        stats_affine(j)
-        for i, h in enumerate(tile_order):
-            norm_store(j, h, ("vector", "scalar", "gpsimd")[i % 3])
+        finish_stats(j)
+        norm_store(j - 1, tile_order[NHB - 2], "vector")
+        stats_scale(j)
+        for i, tile in enumerate(tile_order):
+            norm_store(j, tile, "scalar" if i % 3 == 1 else "vector")
+            if i == 2:
+                norm_store(j - 1, tile_order[NHB - 1], "vector")

@@ -27,7 +27,10 @@ EPS = 1e-5
 
 HB = 1024
 NHB = NT // HB
+PE_FROM = 2
 X_SCALAR = 320
+X_PIECES = (256, 128)
+X_TENSOR = sum(X_PIECES)
 WO_AT = 12
 G_NORM = (7, 7, 6)
 S_NORM_AT = 5
@@ -44,7 +47,8 @@ def tile_nonlocallayer_pa_t_kernel(tc, inputs, Wv, bv, row, Wo, bo, gamma, beta,
         work = ctx.enter_context(tc.tile_pool(name="work", bufs=2))
         resp = ctx.enter_context(tc.tile_pool(name="resp", bufs=16))
         stat = ctx.enter_context(tc.tile_pool(name="stat", bufs=2))
-        psum = ctx.enter_context(tc.psum_pool(name="psum", bufs=8))
+        psum = ctx.enter_context(tc.psum_pool(name="psum", bufs=6))
+        psumx = ctx.enter_context(tc.psum_pool(name="psumx", bufs=2))
         ctx.enter_context(tc.manual_schedule())
 
         x_sb = [keep.tile([P, PACK, CH], BF16, name="x%d" % k) for k in range(NCHUNK)]
@@ -56,6 +60,7 @@ def tile_nonlocallayer_pa_t_kernel(tc, inputs, Wv, bv, row, Wo, bo, gamma, beta,
         wq = [keep.tile([P, 512], U32, name="wq%d" % s, align_bytes=64) for s in range(2)]
         ws = [keep.tile([P, 512], U8, name="ws%d" % s, align_bytes=64) for s in range(2)]
         ident = keep.tile([P, P], F32, name="ident")
+        ident_b = keep.tile([P, P], BF16, name="ident_b")
         bv_b = keep.tile([P, PACK], BF16, name="bv_b")
         bo_b = keep.tile([P, PACK], BF16, name="bo_b")
         ga_b = keep.tile([P, PACK], BF16, name="ga_b")
@@ -77,6 +82,7 @@ def tile_nonlocallayer_pa_t_kernel(tc, inputs, Wv, bv, row, Wo, bo, gamma, beta,
         for j in range(PACK):
             nc.vector.tensor_scalar(out=sqs[:, j, 0:1], in0=one[:], scalar1=NT * EPS, scalar2=None, op0=ALU.mult)
         make_identity(nc, ident[:])
+        make_identity(nc, ident_b[:])
         nc.vector.memset(ones[:], 1.0)
 
         raw = [resp.tile([P, HB], F32, name="raw%d" % s, tag="res") for s in range(2)]
@@ -123,8 +129,9 @@ def tile_nonlocallayer_pa_t_kernel(tc, inputs, Wv, bv, row, Wo, bo, gamma, beta,
         def w_copy(s):
             wg[s] = work.tile([P, PACK * 512], BF16, name="gw%d" % s, tag="gv", bufs=3, align_bytes=64)
             g4 = wg[s][:].bitcast(F32).rearrange("p (h i m u) -> p h i m u", h=2, i=2, u=2)
+            copy = nc.vector.tensor_copy if s == 0 else nc.scalar.copy
             for h in range(2):
-                nc.vector.tensor_copy(out=g4[:, h], in_=wps[(s, h)].rearrange("p i u m -> p i m u"))
+                copy(out=g4[:, h], in_=wps[(s, h)].rearrange("p i u m -> p i m u"))
 
         def w_quant(s):
             nc.vector.quantize_mx(out=wq[s][:].bitcast(FP8X4), scales=ws[s][:], in_=wg[s][:])
@@ -154,12 +161,34 @@ def tile_nonlocallayer_pa_t_kernel(tc, inputs, Wv, bv, row, Wo, bo, gamma, beta,
         def rows_view(src):
             return src.rearrange("p t (c i) -> p c t i", i=4)
 
+        xp = {}
+
+        def tensor_regroup_x(k):
+            xp[k] = []
+            c0 = 0
+            for width in X_PIECES:
+                ps = psumx.tile([P, PACK * width], BF16, name="xp", tag="xp")
+                xp[k].append(ps)
+                view = ps[:].rearrange("p (c u t) -> p u c t", u=2, t=2)
+                for u in range(2):
+                    nc.tensor.matmul(out=view[:, u], lhsT=ident_b[:],
+                                     rhs=x_sb[k][:, 2 * u:2 * u + 2, c0:c0 + width].rearrange("p t c -> p c t"),
+                                     start=True, stop=True)
+                c0 += width
+
         def regroup_x(k):
             gx[k] = work.tile([P, PACK * CH], BF16, name="gx", align_bytes=64)
-            nc.scalar.copy(out=grouped_view(gx[k][:, 0:PACK * X_SCALAR]),
-                           in_=rows_view(x_sb[k][:, :, 0:X_SCALAR]))
-            nc.gpsimd.tensor_scalar(out=grouped_view(gx[k][:, PACK * X_SCALAR:PACK * CH]),
-                                    in0=rows_view(x_sb[k][:, :, X_SCALAR:CH]),
+            if k < PE_FROM:
+                rest = X_SCALAR
+                nc.scalar.copy(out=grouped_view(gx[k][:, 0:PACK * rest]), in_=rows_view(x_sb[k][:, :, 0:rest]))
+            else:
+                rest = X_TENSOR
+                c0 = 0
+                for width, ps in zip(X_PIECES, xp[k]):
+                    nc.scalar.copy(out=gx[k][:, PACK * c0:PACK * (c0 + width)], in_=ps[:])
+                    c0 += width
+            nc.gpsimd.tensor_scalar(out=grouped_view(gx[k][:, PACK * rest:PACK * CH]),
+                                    in0=rows_view(x_sb[k][:, :, rest:CH]),
                                     scalar1=1.0, scalar2=0.0, op0=ALU.mult, op1=ALU.add)
 
         def quant_x(k):
@@ -181,7 +210,10 @@ def tile_nonlocallayer_pa_t_kernel(tc, inputs, Wv, bv, row, Wo, bo, gamma, beta,
         def gate(k):
             b, cols = where(k)
             zt[k] = work.tile([P, PACK, CH], BF16, name="z", tag="z", bufs=3)
-            for t in range(PACK) if k < 2 else reversed(range(PACK)):
+            order = list(range(PACK))
+            if k >= 2:
+                order = order[-1:] + order[:-1]
+            for t in order:
                 nc.vector.scalar_tensor_tensor(out=zt[k][:, t, :], in0=ps1[k][t][:], scalar=bv_f[:, t:t + 1],
                                                in1=rowb[:, b, cols], op0=ALU.add, op1=ALU.mult)
 
@@ -199,7 +231,8 @@ def tile_nonlocallayer_pa_t_kernel(tc, inputs, Wv, bv, row, Wo, bo, gamma, beta,
         ps2 = {}
 
         def matmul_2(j, k):
-            ps2[(j, k)] = psum.tile([P, CH], F32, name="ps2", tag="ps")
+            pool, tag = (psumx, "xp") if k % GROUP == 0 else (psum, "ps")
+            ps2[(j, k)] = pool.tile([P, CH], F32, name="ps2", tag=tag)
             nc.tensor.matmul_mx(out=ps2[(j, k)][:], lhsT=wq[1][:, j * P:(j + 1) * P].bitcast(FP8X4),
                                 lhsT_scale=ws[1][:, j * P:(j + 1) * P],
                                 rhs=vq[:, k * CH:(k + 1) * CH].bitcast(FP8X4),
@@ -325,12 +358,15 @@ def tile_nonlocallayer_pa_t_kernel(tc, inputs, Wv, bv, row, Wo, bo, gamma, beta,
                 matmul_1(i + 1)
             if i + 2 < NCHUNK:
                 regroup_x(i + 2)
+            if PE_FROM <= i + 3 < NCHUNK and i != WO_AT:
+                tensor_regroup_x(i + 3)
             if 1 <= i <= NCHUNK:
                 relu_regroup(i - 1)
             if 1 <= i < NCHUNK:
                 gate(i)
             if i == WO_AT:
                 matmul_1(i + 1)
+                tensor_regroup_x(i + 3)
                 w_copy(1)
             if i == WO_AT + 2:
                 nc.gpsimd.tensor_scalar(out=negbo[:], in0=bo_b[:], scalar1=-1.0, scalar2=0.0, op0=ALU.mult, op1=ALU.add)

@@ -27,8 +27,8 @@ EPS = 1e-5
 
 HB = 1024
 NHB = NT // HB
-PE_FROM = 2
-X_SCALAR = 320
+PE_FROM = 3
+X_SCALAR = (384, 320, 320)
 X_PIECES = (256, 128)
 X_TENSOR = sum(X_PIECES)
 WO_AT = 12
@@ -179,7 +179,7 @@ def tile_nonlocallayer_pa_t_kernel(tc, inputs, Wv, bv, row, Wo, bo, gamma, beta,
         def regroup_x(k):
             gx[k] = work.tile([P, PACK * CH], BF16, name="gx", align_bytes=64)
             if k < PE_FROM:
-                rest = X_SCALAR
+                rest = X_SCALAR[k]
                 nc.scalar.copy(out=grouped_view(gx[k][:, 0:PACK * rest]), in_=rows_view(x_sb[k][:, :, 0:rest]))
             else:
                 rest = X_TENSOR
@@ -349,24 +349,24 @@ def tile_nonlocallayer_pa_t_kernel(tc, inputs, Wv, bv, row, Wo, bo, gamma, beta,
                 nc.vector.tensor_copy(out=bv_f[:], in_=bv_b[:])
                 copy_row(nc.vector.tensor_copy, 0)
                 gate(0)
-                copy_row(nc.scalar.copy, 1)
             if 0 <= i + 1 < NCHUNK:
                 quant_x(i + 1)
+            if i + 2 < NCHUNK:
+                regroup_x(i + 2)
+            if i == 0:
+                copy_row(nc.scalar.copy, 1)
+            if PE_FROM <= i + 3 < NCHUNK:
+                tensor_regroup_x(i + 3)
             if i == WO_AT:
                 w_transpose(1)
             elif 0 <= i + 1 < NCHUNK:
                 matmul_1(i + 1)
-            if i + 2 < NCHUNK:
-                regroup_x(i + 2)
-            if PE_FROM <= i + 3 < NCHUNK and i != WO_AT:
-                tensor_regroup_x(i + 3)
             if 1 <= i <= NCHUNK:
                 relu_regroup(i - 1)
             if 1 <= i < NCHUNK:
                 gate(i)
             if i == WO_AT:
                 matmul_1(i + 1)
-                tensor_regroup_x(i + 3)
                 w_copy(1)
             if i == WO_AT + 2:
                 nc.gpsimd.tensor_scalar(out=negbo[:], in0=bo_b[:], scalar1=-1.0, scalar2=0.0, op0=ALU.mult, op1=ALU.add)
@@ -381,7 +381,7 @@ def tile_nonlocallayer_pa_t_kernel(tc, inputs, Wv, bv, row, Wo, bo, gamma, beta,
                 stage_2(0, 0)
             if i >= 2:
                 quant_v(i - 2)
-            if i == WO_AT:
+            if i == WO_AT + 1:
                 w_quant(1)
         for j in range(PACK):
             for g in range(1 if j == 0 else 0, NCHUNK // GROUP):

@@ -31,7 +31,9 @@ PE_FROM = 3
 X_SCALAR = (384, 320, 320)
 X_PIECES = (256, 128)
 X_TENSOR = sum(X_PIECES)
-WO_AT = 12
+SHARED = range(4, 14, 2)
+WO_AT = 13
+CONSTANTS_AT = 10
 G_NORM = (7, 7, 6)
 S_NORM_AT = 5
 GROUP = 4
@@ -120,7 +122,7 @@ def tile_nonlocallayer_pa_t_kernel(tc, inputs, Wv, bv, row, Wo, bo, gamma, beta,
         def w_transpose(s):
             words = raw[s][:].rearrange("p (i q u) -> p i u q", i=PACK, u=2)
             for h in range(2):
-                ps = psum.tile([P, 512], F32, name="pst", tag="ps")
+                ps = (psum if s == 0 else psumx).tile([P, 512], F32, name="pst", tag="ps" if s == 0 else "xp")
                 wps[(s, h)] = ps[:].rearrange("p (i u m) -> p i u m", i=2, u=2)
                 for i2 in range(2):
                     for u in range(2):
@@ -209,13 +211,21 @@ def tile_nonlocallayer_pa_t_kernel(tc, inputs, Wv, bv, row, Wo, bo, gamma, beta,
 
         def gate(k):
             b, cols = where(k)
-            zt[k] = work.tile([P, PACK, CH], BF16, name="z", tag="z", bufs=3)
+            if k not in SHARED:
+                zt[k] = work.tile([P, PACK, CH], BF16, name="z", tag="z", bufs=3)
             order = list(range(PACK))
             if k >= 2:
-                order = order[-1:] + order[:-1]
+                order = order[-1:] + order[1 if k in SHARED else 0:-1]
             for t in order:
                 nc.vector.scalar_tensor_tensor(out=zt[k][:, t, :], in0=ps1[k][t][:], scalar=bv_f[:, t:t + 1],
                                                in1=rowb[:, b, cols], op0=ALU.add, op1=ALU.mult)
+
+        def gate_shared(k):
+            b, cols = where(k)
+            zt[k] = work.tile([P, PACK, CH], BF16, name="z", tag="z", bufs=3)
+            y = work.tile([P, CH], F32, name="y")
+            nc.scalar.activation(out=y[:], in_=ps1[k][0][:], func=ACT.Identity, bias=bv_f[:, 0:1], scale=1.0)
+            nc.gpsimd.tensor_tensor(out=zt[k][:, 0, :], in0=y[:], in1=rowb[:, b, cols], op=ALU.mult)
 
         def relu_regroup(k):
             gv[k] = work.tile([P, PACK * CH], BF16, name="gv", tag="gv", bufs=3, align_bytes=64)
@@ -351,6 +361,8 @@ def tile_nonlocallayer_pa_t_kernel(tc, inputs, Wv, bv, row, Wo, bo, gamma, beta,
                 gate(0)
             if 0 <= i + 1 < NCHUNK:
                 quant_x(i + 1)
+            if i in SHARED:
+                gate_shared(i)
             if i + 2 < NCHUNK:
                 regroup_x(i + 2)
             if i == 0:
@@ -359,23 +371,22 @@ def tile_nonlocallayer_pa_t_kernel(tc, inputs, Wv, bv, row, Wo, bo, gamma, beta,
                 tensor_regroup_x(i + 3)
             if i == WO_AT:
                 w_transpose(1)
-            elif 0 <= i + 1 < NCHUNK:
+            if 0 <= i + 1 < NCHUNK:
                 matmul_1(i + 1)
             if 1 <= i <= NCHUNK:
                 relu_regroup(i - 1)
             if 1 <= i < NCHUNK:
                 gate(i)
             if i == WO_AT:
-                matmul_1(i + 1)
                 w_copy(1)
-            if i == WO_AT + 2:
+            if i == CONSTANTS_AT:
                 nc.gpsimd.tensor_scalar(out=negbo[:], in0=bo_b[:], scalar1=-1.0, scalar2=0.0, op0=ALU.mult, op1=ALU.add)
                 nc.gpsimd.tensor_scalar(out=minbo[:], in0=bo_b[:], scalar1=0.0, scalar2=0.0, op0=ALU.min, op1=ALU.add)
                 nc.gpsimd.tensor_scalar(out=ga_f[:], in0=ga_b[:], scalar1=1.0, scalar2=0.0, op0=ALU.mult, op1=ALU.add)
                 nc.gpsimd.tensor_scalar(out=ga_n[:], in0=ga_b[:], scalar1=float(NT), scalar2=0.0,
                                         op0=ALU.mult, op1=ALU.add)
                 nc.gpsimd.tensor_scalar(out=be_f[:], in0=be_b[:], scalar1=1.0, scalar2=0.0, op0=ALU.mult, op1=ALU.add)
-            if i == WO_AT + 3:
+            if i == CONSTANTS_AT + 1:
                 nc.scalar.activation(out=sums[:, :, 0:1], in_=minbo[:].unsqueeze(2), func=ACT.Copy, scale=float(NT))
             if i == NCHUNK + 1:
                 stage_2(0, 0)

from contextlib import ExitStack

import concourse.mybir as mybir
from concourse.masks import make_identity

FLOPS = 2 * 2 * 512 * 512 * 8192

BF16 = mybir.dt.bfloat16
F32 = mybir.dt.float32
U32 = mybir.dt.uint32
U8 = mybir.dt.uint8
I32 = mybir.dt.int32
FP8X4 = mybir.dt.float8_e4m3fn_x4
ALU = mybir.AluOpType
ACT = mybir.ActivationFunctionType
AX = mybir.AxisListType

P = 128
PACK = 4
B = 4
N = 2048
CH = 512
QB = N // CH
NCHUNK = B * QB
NT = B * N
EPS = 1e-5

HB = 1024
NHB = NT // HB
PE_FROM = 3
X_SCALAR = (384, 320, 320)
X_PIECES = (256, 128)
X_TENSOR = sum(X_PIECES)
SHARED = range(4, 14, 2)
WO_AT = 13
CONSTANTS_AT = 10
G_NORM = (7, 7, 6)
S_NORM_AT = 5
GROUP = 4


def tile_nonlocallayer_pa_t_kernel(tc, inputs, Wv, bv, row, Wo, bo, gamma, beta, out):
    nc = tc.nc
    xv = inputs.rearrange("b (p j) t h w -> b p j (t h w)", j=PACK)
    ov = out.rearrange("b (p j) t h w -> b p j (t h w)", j=PACK)

    with ExitStack() as ctx:
        keep = ctx.enter_context(tc.tile_pool(name="keep", bufs=1))
        work = ctx.enter_context(tc.tile_pool(name="work", bufs=2))
        resp = ctx.enter_context(tc.tile_pool(name="resp", bufs=16))
        stat = ctx.enter_context(tc.tile_pool(name="stat", bufs=2))
        psum = ctx.enter_context(tc.psum_pool(name="psum", bufs=6))
        psumx = ctx.enter_context(tc.psum_pool(name="psumx", bufs=2))
        ctx.enter_context(tc.manual_schedule())

        x_sb = [keep.tile([P, PACK, CH], BF16, name="x%d" % k) for k in range(NCHUNK)]
        rowb = keep.tile([P, B, N], BF16, name="rowb")
        rsrc = keep.tile([P, HB], BF16, name="rsrc")
        ones = keep.tile([P, P], BF16, name="ones")
        vq = keep.tile([P, NT], U32, name="vq", align_bytes=64)
        vs = keep.tile([P, NT], U8, name="vs", align_bytes=64)
        wq = [keep.tile([P, 512], U32, name="wq%d" % s, align_bytes=64) for s in range(2)]
        ws = [keep.tile([P, 512], U8, name="ws%d" % s, align_bytes=64) for s in range(2)]
        ident = keep.tile([P, P], F32, name="ident")
        ident_b = keep.tile([P, P], BF16, name="ident_b")
        bv_b = keep.tile([P, PACK], BF16, name="bv_b")
        bo_b = keep.tile([P, PACK], BF16, name="bo_b")
        ga_b = keep.tile([P, PACK], BF16, name="ga_b")
        be_b = keep.tile([P, PACK], BF16, name="be_b")
        bv_f = keep.tile([P, PACK], F32, name="bv_f")
        negbo = keep.tile([P, PACK], F32, name="negbo")
        minbo = keep.tile([P, PACK], F32, name="minbo")
        ga_f = keep.tile([P, PACK], F32, name="ga_f")
        ga_n = keep.tile([P, PACK], F32, name="ga_n")
        be_f = keep.tile([P, PACK], F32, name="be_f")
        sums = keep.tile([P, PACK, 1 + NCHUNK], F32, name="sums")
        sqs = keep.tile([P, PACK, 1 + NHB + 1], F32, name="sqs")
        one = keep.tile([P, 1], F32, name="one")
        one_s = keep.tile([P, 1], F32, name="one_s")

        nc.vector.memset(rsrc[:].bitcast(I32), 0)
        nc.vector.memset(one[:], 1.0)
        nc.scalar.activation(out=one_s[:], in_=one[:], func=ACT.Abs_reciprocal_sqrt)
        for j in range(PACK):
            nc.vector.tensor_scalar(out=sqs[:, j, 0:1], in0=one[:], scalar1=NT * EPS, scalar2=None, op0=ALU.mult)
        make_identity(nc, ident[:])
        make_identity(nc, ident_b[:])
        nc.vector.memset(ones[:], 1.0)

        raw = [resp.tile([P, HB], F32, name="raw%d" % s, tag="res") for s in range(2)]

        def load_x(k):
            b, q = divmod(k, QB)
            nc.sync.dma_start(out=x_sb[k][:], in_=xv[b][:, :, q * CH:(q + 1) * CH])

        def load_vec(dst, src):
            nc.sync.dma_start(out=dst[:], in_=src.rearrange("(p i) -> p i", i=PACK))

        def load_w(s, w):
            nc.sync.dma_start(out=raw[s][:].bitcast(BF16).rearrange("p (i c) -> p i c", i=PACK),
                              in_=w.rearrange("(m i) c -> m i c", i=PACK))

        load_w(0, Wv)
        load_x(0)
        nc.sync.dma_start(out=rsrc[0:1, :], in_=row[0:1, 0:HB])
        load_vec(bv_b, bv)
        for k in range(1, QB):
            load_x(k)
        nc.sync.dma_start(out=rowb[:, 0, HB:N], in_=row[0, HB:N].partition_broadcast(P))
        for b in range(1, B):
            for q in range(QB):
                load_x(b * QB + q)
            nc.sync.dma_start(out=rowb[:, b, :], in_=row[b, :].partition_broadcast(P))
        load_w(1, Wo)
        load_vec(bo_b, bo)
        load_vec(ga_b, gamma)
        load_vec(be_b, beta)

        wps = {}
        wg = {}

        def w_transpose(s):
            words = raw[s][:].rearrange("p (i q u) -> p i u q", i=PACK, u=2)
            for h in range(2):
                ps = (psum if s == 0 else psumx).tile([P, 512], F32, name="pst", tag="ps" if s == 0 else "xp")
                wps[(s, h)] = ps[:].rearrange("p (i u m) -> p i u m", i=2, u=2)
                for i2 in range(2):
                    for u in range(2):
                        nc.tensor.transpose(wps[(s, h)][:, i2, u, :], words[:, 2 * h + i2, u, :], ident[:])

        def w_copy(s):
            wg[s] = work.tile([P, PACK * 512], BF16, name="gw%d" % s, tag="gv", bufs=3, align_bytes=64)
            g4 = wg[s][:].bitcast(F32).rearrange("p (h i m u) -> p h i m u", h=2, i=2, u=2)
            copy = nc.vector.tensor_copy if s == 0 else nc.scalar.copy
            for h in range(2):
                copy(out=g4[:, h], in_=wps[(s, h)].rearrange("p i u m -> p i m u"))

        def w_quant(s):
            nc.vector.quantize_mx(out=wq[s][:].bitcast(FP8X4), scales=ws[s][:], in_=wg[s][:])

        rps = psum.tile([P, HB], BF16, name="rps", tag="ps")

        def spread_row():
            for c0 in range(0, HB, CH):
                nc.tensor.matmul(out=rps[:, c0:c0 + CH], lhsT=ones[:], rhs=rsrc[:, c0:c0 + CH], start=True, stop=True)

        def copy_row(engine_copy, k):
            engine_copy(out=rowb[:, 0, k * CH:(k + 1) * CH], in_=rps[:, k * CH:(k + 1) * CH])

        gx = {}
        xq = {}
        ps1 = {}
        zt = {}
        gv = {}

        def where(k):
            b, q = divmod(k, QB)
            return b, slice(q * CH, (q + 1) * CH)

        def grouped_view(dst):
            return dst.rearrange("p (c i t) -> p c t i", i=4, t=PACK)

        def rows_view(src):
            return src.rearrange("p t (c i) -> p c t i", i=4)

        xp = {}

        def tensor_regroup_x(k):
            xp[k] = []
            c0 = 0
            for width in X_PIECES:
                ps = psumx.tile([P, PACK * width], BF16, name="xp", tag="xp")
                xp[k].append(ps)
                view = ps[:].rearrange("p (c u t) -> p u c t", u=2, t=2)
                for u in range(2):
                    nc.tensor.matmul(out=view[:, u], lhsT=ident_b[:],
                                     rhs=x_sb[k][:, 2 * u:2 * u + 2, c0:c0 + width].rearrange("p t c -> p c t"),
                                     start=True, stop=True)
                c0 += width

        def regroup_x(k):
            gx[k] = work.tile([P, PACK * CH], BF16, name="gx", align_bytes=64)
            if k < PE_FROM:
                rest = X_SCALAR[k]
                nc.scalar.copy(out=grouped_view(gx[k][:, 0:PACK * rest]), in_=rows_view(x_sb[k][:, :, 0:rest]))
            else:
                rest = X_TENSOR
                c0 = 0
                for width, ps in zip(X_PIECES, xp[k]):
                    nc.scalar.copy(out=gx[k][:, PACK * c0:PACK * (c0 + width)], in_=ps[:])
                    c0 += width
            nc.gpsimd.tensor_scalar(out=grouped_view(gx[k][:, PACK * rest:PACK * CH]),
                                    in0=rows_view(x_sb[k][:, :, rest:CH]),
                                    scalar1=1.0, scalar2=0.0, op0=ALU.mult, op1=ALU.add)

        def quant_x(k):
            codes = work.tile([P, CH], U32, name="xq", align_bytes=64)
            scales = work.tile([P, CH], U8, name="xs", align_bytes=64)
            xq[k] = (codes, scales)
            nc.vector.quantize_mx(out=codes[:].bitcast(FP8X4), scales=scales[:], in_=gx[k][:])

        def matmul_1(k):
            codes, scales = xq[k]
            ps1[k] = []
            for t in range(PACK):
                ps = psum.tile([P, CH], F32, name="ps1", tag="ps")
                ps1[k].append(ps)
                nc.tensor.matmul_mx(out=ps[:], lhsT=wq[0][:, t * P:(t + 1) * P].bitcast(FP8X4),
                                    lhsT_scale=ws[0][:, t * P:(t + 1) * P],
                                    rhs=codes[:].bitcast(FP8X4), rhs_scale=scales[:], start=True, stop=True)

        def gate(k):
            b, cols = where(k)
            if k not in SHARED:
                zt[k] = work.tile([P, PACK, CH], BF16, name="z", tag="z", bufs=3)
            order = list(range(PACK))
            if k >= 2:
                order = order[-1:] + order[1 if k in SHARED else 0:-1]
            for t in order:
                nc.vector.scalar_tensor_tensor(out=zt[k][:, t, :], in0=ps1[k][t][:], scalar=bv_f[:, t:t + 1],
                                               in1=rowb[:, b, cols], op0=ALU.add, op1=ALU.mult)

        def gate_shared(k):
            b, cols = where(k)
            zt[k] = work.tile([P, PACK, CH], BF16, name="z", tag="z", bufs=3)
            y = work.tile([P, CH], F32, name="y")
            nc.scalar.activation(out=y[:], in_=ps1[k][0][:], func=ACT.Identity, bias=bv_f[:, 0:1], scale=1.0)
            nc.gpsimd.tensor_tensor(out=zt[k][:, 0, :], in0=y[:], in1=rowb[:, b, cols], op=ALU.mult)

        def relu_regroup(k):
            gv[k] = work.tile([P, PACK * CH], BF16, name="gv", tag="gv", bufs=3, align_bytes=64)
            nc.scalar.activation(out=grouped_view(gv[k][:]), in_=rows_view(zt[k][:]), func=ACT.Relu)

        def quant_v(k):
            nc.vector.quantize_mx(out=vq[:, k * CH:(k + 1) * CH].bitcast(FP8X4),
                                  scales=vs[:, k * CH:(k + 1) * CH], in_=gv[k][:])

        res = {}
        st = {}

        ps2 = {}

        def matmul_2(j, k):
            pool, tag = (psumx, "xp") if k % GROUP == 0 else (psum, "ps")
            ps2[(j, k)] = pool.tile([P, CH], F32, name="ps2", tag=tag)
            nc.tensor.matmul_mx(out=ps2[(j, k)][:], lhsT=wq[1][:, j * P:(j + 1) * P].bitcast(FP8X4),
                                lhsT_scale=ws[1][:, j * P:(j + 1) * P],
                                rhs=vq[:, k * CH:(k + 1) * CH].bitcast(FP8X4),
                                rhs_scale=vs[:, k * CH:(k + 1) * CH], start=True, stop=True)

        def join(j, k, n):
            h, half = divmod(k, HB // CH)
            if n % (HB // CH) == 0:
                res[(j, h)] = resp.tile([P, HB], F32, name="res", tag="res")
            nc.vector.scalar_tensor_tensor(out=res[(j, h)][:, half * CH:(half + 1) * CH], in0=ps2[(j, k)][:],
                                           scalar=negbo[:, j:j + 1], in1=x_sb[k][:, j, :],
                                           op0=ALU.max, op1=ALU.add, accum_out=sums[:, j, 1 + n:2 + n])

        def squares(j, h, c0, c1, slot):
            nc.scalar.activation(out=rowb[:, 0, c0:c1], in_=res[(j, h)][:, c0:c1], func=ACT.Square,
                                 bias=minbo[:, j:j + 1], scale=1.0, accum_out=sqs[:, j, 1 + slot:2 + slot])

        def small(j, name):
            st[(j, name)] = stat.tile([P, 1], F32, name=name)
            return st[(j, name)]

        def stats_sum(j):
            nc.vector.tensor_reduce(out=small(j, "s1_part")[:], in_=sums[:, j, 0:NCHUNK - 1], axis=AX.X, op=ALU.add)

        def stats_total(j):
            nc.vector.tensor_reduce(out=small(j, "s2_part")[:], in_=sqs[:, j, 0:NHB], axis=AX.X, op=ALU.add)
            nc.vector.scalar_tensor_tensor(out=small(j, "s1")[:], in0=sums[:, j, NCHUNK:NCHUNK + 1],
                                           scalar=sums[:, j, NCHUNK - 1:NCHUNK], in1=st[(j, "s1_part")][:],
                                           op0=ALU.add, op1=ALU.add)

        def stats_square(j):
            nc.vector.tensor_scalar(out=small(j, "s2_n")[:], in0=sqs[:, j, NHB:NHB + 1], scalar1=st[(j, "s2_part")][:],
                                    scalar2=float(NT), op0=ALU.add, op1=ALU.mult)

        def stats_mean(j):
            nc.vector.scalar_tensor_tensor(out=small(j, "mean_n")[:], in0=sums[:, j, 0:1], scalar=st[(j, "s1")][:],
                                           in1=ga_f[:, j:j + 1], op0=ALU.subtract, op1=ALU.mult)

        def stats_base(j):
            nc.vector.scalar_tensor_tensor(out=small(j, "base")[:], in0=st[(j, "s1")][:], scalar=st[(j, "s1")][:],
                                           in1=st[(j, "s2_n")][:], op0=ALU.mult, op1=ALU.subtract)

        def stats_affine(j):
            rstd = small(j, "rstd")
            nc.scalar.activation(out=rstd[:], in_=sqs[:, j, NHB + 1:NHB + 2], func=ACT.Abs_reciprocal_sqrt,
                                 bias=st[(j, "base")][:], scale=-float(NT))
            if j == PACK - 1:
                nc.scalar.activation(out=small(j, "sh")[:], in_=rstd[:], func=ACT.Identity, bias=be_f[:, j:j + 1],
                                     scale=st[(j, "mean_n")][:])
            else:
                nc.gpsimd.tensor_scalar(out=small(j, "sc")[:], in0=rstd[:], scalar1=ga_n[:, j:j + 1], scalar2=0.0,
                                        op0=ALU.mult, op1=ALU.add)
                nc.gpsimd.tensor_scalar(out=small(j, "sh")[:], in0=rstd[:], scalar1=st[(j, "mean_n")][:],
                                        scalar2=be_f[:, j:j + 1], op0=ALU.mult, op1=ALU.add)

        def stats_scale(j):
            nc.vector.tensor_scalar(out=small(j, "sc")[:], in0=st[(j, "rstd")][:], scalar1=ga_n[:, j:j + 1],
                                    scalar2=None, op0=ALU.mult)

        def norm_store(j, h, engine):
            r = res[(j, h)]
            sc = st[(j, "sc")]
            sh = st[(j, "sh")]
            if engine == "scalar":
                nc.scalar.activation(out=r[:], in_=r[:], func=ACT.Identity, bias=sh[:, 0:1], scale=sc[:, 0:1])
            elif engine == "vector":
                nc.vector.tensor_scalar(out=r[:], in0=r[:], scalar1=sc[:, 0:1], scalar2=sh[:, 0:1],
                                        op0=ALU.mult, op1=ALU.add)
            else:
                nc.gpsimd.tensor_scalar(out=r[:], in0=r[:], scalar1=sc[:, 0:1], scalar2=sh[:, 0:1],
                                        op0=ALU.mult, op1=ALU.add)
            b, half = divmod(h, N // HB)
            nc.sync.dma_start(out=ov[b][:, j, half * HB:(half + 1) * HB], in_=r[:])

        def finish_stats(j):
            stats_total(j)
            stats_square(j)
            stats_mean(j)
            stats_base(j)
            stats_affine(j)

        chunk_order = [g0 + GROUP - 1 - i for g0 in range(0, NCHUNK, GROUP) for i in range(GROUP)]
        tile_order = [chunk_order[n] * CH // HB for n in range(0, NCHUNK, HB // CH)]

        def after_join(j, k, n):
            if j >= 1 and n == 1:
                finish_stats(j - 1)
                for tile in tile_order[0:G_NORM[j - 1]]:
                    norm_store(j - 1, tile, "gpsimd")
            if 1 <= j < PACK - 1 and n == S_NORM_AT:
                norm_store(j - 1, tile_order[NHB - 1], "scalar")
            h, half = divmod(k, HB // CH)
            if n >= NCHUNK - 2:
                squares(j, h, half * CH, (half + 1) * CH, n - NHB + 1)
            elif n % 2 == 1:
                squares(j, h, 0, HB, n // 2)
            if n == NCHUNK - 2:
                stats_sum(j)

        def stage_2(j, g):
            ks = chunk_order[g * GROUP:(g + 1) * GROUP]
            for k in reversed(ks):
                matmul_2(j, k)
            for i, k in enumerate(ks):
                join(j, k, g * GROUP + i)
                after_join(j, k, g * GROUP + i)

        w_transpose(0)
        spread_row()
        w_copy(0)
        w_quant(0)
        for i in range(-2, NCHUNK + 2):
            if i == 0:
                nc.vector.tensor_copy(out=bv_f[:], in_=bv_b[:])
                copy_row(nc.vector.tensor_copy, 0)
                gate(0)
            if 0 <= i + 1 < NCHUNK:
                quant_x(i + 1)
            if i in SHARED:
                gate_shared(i)
            if i + 2 < NCHUNK:
                regroup_x(i + 2)
            if i == 0:
                copy_row(nc.scalar.copy, 1)
            if PE_FROM <= i + 3 < NCHUNK:
                tensor_regroup_x(i + 3)
            if i == WO_AT:
                w_transpose(1)
            if 0 <= i + 1 < NCHUNK:
                matmul_1(i + 1)
            if 1 <= i <= NCHUNK:
                relu_regroup(i - 1)
            if 1 <= i < NCHUNK:
                gate(i)
            if i == WO_AT:
                w_copy(1)
            if i == CONSTANTS_AT:
                nc.gpsimd.tensor_scalar(out=negbo[:], in0=bo_b[:], scalar1=-1.0, scalar2=0.0, op0=ALU.mult, op1=ALU.add)
                nc.gpsimd.tensor_scalar(out=minbo[:], in0=bo_b[:], scalar1=0.0, scalar2=0.0, op0=ALU.min, op1=ALU.add)
                nc.gpsimd.tensor_scalar(out=ga_f[:], in0=ga_b[:], scalar1=1.0, scalar2=0.0, op0=ALU.mult, op1=ALU.add)
                nc.gpsimd.tensor_scalar(out=ga_n[:], in0=ga_b[:], scalar1=float(NT), scalar2=0.0,
                                        op0=ALU.mult, op1=ALU.add)
                nc.gpsimd.tensor_scalar(out=be_f[:], in0=be_b[:], scalar1=1.0, scalar2=0.0, op0=ALU.mult, op1=ALU.add)
            if i == CONSTANTS_AT + 1:
                nc.scalar.activation(out=sums[:, :, 0:1], in_=minbo[:].unsqueeze(2), func=ACT.Copy, scale=float(NT))
            if i == NCHUNK + 1:
                stage_2(0, 0)
            if i >= 2:
                quant_v(i - 2)
            if i == WO_AT + 1:
                w_quant(1)
        for j in range(PACK):
            for g in range(1 if j == 0 else 0, NCHUNK // GROUP):
                stage_2(j, g)
        j = PACK - 1
        finish_stats(j)
        norm_store(j - 1, tile_order[NHB - 2], "vector")
        stats_scale(j)
        for i, tile in enumerate(tile_order):
            norm_store(j, tile, "scalar" if i % 3 == 1 else "vector")
            if i == 2:
                norm_store(j - 1, tile_order[NHB - 1], "vector")
